import numpy as np
import ml_dtypes


def mxq(x, axis, fmt="e4m3"):
    dtype, down = {"e4m3": (ml_dtypes.float8_e4m3fn, 7), "e5m2": (ml_dtypes.float8_e5m2, 14)}[fmt]
    v = np.moveaxis(np.asarray(x, np.float32).astype(ml_dtypes.bfloat16).astype(np.float64), axis, -1)
    blocks = v.reshape(v.shape[:-1] + (-1, 32))
    amax = np.abs(blocks).max(-1, keepdims=True)
    byte = np.maximum(np.where(amax > 0, np.frexp(amax)[1] - 1 + 127, 0) - down, 1)
    scale = np.exp2(byte - 127.0)
    codes = (blocks / scale).astype(np.float32).astype(dtype).astype(np.float64)
    return np.moveaxis((codes * scale).reshape(v.shape), -1, axis)


WIDE = False


def mx_kscale(k):
    if not WIDE:
        return np.ones(k)
    levels = np.array([10, -10, 5, -5, 0])
    a = np.random.permutation(np.resize(levels, k // 512 * 4)).reshape(k // 512, 4)
    idx = np.arange(k)
    return np.exp2(a[idx // 512, idx % 128 // 32])


BF16 = ml_dtypes.bfloat16


def bf(x):
    return np.asarray(x, np.float32).astype(BF16)


def f64(x):
    return np.asarray(x).astype(np.float64)


B, H, W, NB, BS, F = 1, 64, 64, 1, 512, 512
C = NB * BS
SPARSITY = 0.01


def blockmm(a, w):
    r = np.moveaxis(a, 3, 0).reshape(NB, B * H * W, -1) @ w
    return np.moveaxis(r, 0, 1).reshape(B, H, W, NB, -1)


def setup_inputs():
    s = mx_kscale(F)
    return {"o1k": bf(np.maximum(np.random.standard_normal((B, H, W, NB, F)), 0.0) * 0.27 * s),
            "o1n": bf(np.maximum(np.random.standard_normal((B, H, W, NB, F)), 0.0) * 0.27 * s),
            "w2": bf(np.random.standard_normal((2, NB, F, BS)) * 0.7 / np.sqrt(F) / s[:, None] * s),
            "b2": bf(np.random.standard_normal((2, NB, BS)) * 0.05 * s)}


def reference(o1k, o1n, w2, b2):
    w2, b2 = f64(w2), f64(b2)
    o1kq = mxq(f64(o1k), 4, "e4m3")
    o1nq = mxq(f64(o1n), 4, "e4m3")
    w2a = mxq(w2[0] + w2[1], 1, "e4m3")
    w2b = mxq(w2[0] - w2[1], 1, "e4m3")
    o2k = 0.5 * (blockmm(o1kq, w2a) + blockmm(o1nq, w2b)) + b2[0]
    o2n = 0.5 * (blockmm(o1nq, w2a) + blockmm(mxq(o2k, 4, "e4m3"), w2b)) + b2[1]
    y = (o2k + o2n).reshape(B, H, W, C)
    return np.sign(y) * np.maximum(np.abs(y) - SPARSITY, 0.0)

@@ -1,0 +1,218 @@
+from contextlib import ExitStack
+
+import concourse.mybir as mybir
+from concourse.masks import make_identity
+
+F32 = mybir.dt.float32
+BF16 = mybir.dt.bfloat16
+U32 = mybir.dt.uint32
+U8 = mybir.dt.uint8
+FP8X4 = mybir.dt.float8_e4m3fn_x4
+ALU = mybir.AluOpType
+ACT = mybir.ActivationFunctionType
+
+P = 128
+PACK = 4
+CH = P * PACK
+TOKENS = 64 * 64
+TILES = TOKENS // P
+ROUND_TILES = 4
+ROUND = ROUND_TILES * P
+ROUNDS = TILES // ROUND_TILES
+THRESHOLD = 0.01
+
+FLOPS = 4 * 2 * TOKENS * CH * CH
+
+
+def tile_afno2d_pb_t_kernel(tc, o1k, o1n, w2, b2, out):
+    nc = tc.nc
+    with ExitStack() as ctx:
+        ctx.enter_context(tc.manual_schedule())
+        keep = ctx.enter_context(tc.tile_pool(name="keep", bufs=1))
+        inputs = ctx.enter_context(tc.tile_pool(name="inputs", bufs=ROUNDS))
+        stage = ctx.enter_context(tc.tile_pool(name="stage", bufs=2))
+        quantised = ctx.enter_context(tc.tile_pool(name="quantised", bufs=4))
+        finish = ctx.enter_context(tc.tile_pool(name="finish", bufs=4))
+        psum = ctx.enter_context(tc.psum_pool(name="psum", bufs=8))
+
+        k_dram = o1k.rearrange("b h w n c -> (b h w n) c").rearrange("(p j) c -> p j c", j=TILES)
+        n_dram = o1n.rearrange("b h w n c -> (b h w n) c").rearrange("(p j) c -> p j c", j=TILES)
+        out_dram = out.rearrange("b h w c -> (b h w) c").rearrange("(p j) c -> p j c", j=TILES)
+
+        bias_rows = keep.tile([P, CH], BF16)
+        nc.vector.memset(bias_rows[:], 0.0)
+        nc.sync.dma_start(out=bias_rows[0:2, :], in_=b2.rearrange("i n c -> (i n) c"))
+
+        w_pairs = keep.tile([P, 2, PACK, CH], BF16)
+        nc.sync.dma_start(
+            out=w_pairs[:].rearrange("p i (u e) c -> p (i u) (e c)", e=2),
+            in_=w2.rearrange("i n (u p e) c -> p (i n u) (e c)", u=2, p=P, e=2),
+        )
+        w_planes = keep.tile([P, 2, PACK, CH], BF16)
+
+        k_rounds = []
+        n_rounds = []
+        for r in range(ROUNDS):
+            tiles_of_round = slice(r * ROUND_TILES, (r + 1) * ROUND_TILES)
+            k_in = inputs.tile([P, ROUND_TILES, CH], BF16)
+            nc.sync.dma_start(out=k_in[:], in_=k_dram[:, tiles_of_round, :])
+            n_in = inputs.tile([P, ROUND_TILES, CH], BF16)
+            nc.sync.dma_start(out=n_in[:], in_=n_dram[:, tiles_of_round, :])
+            k_rounds.append(k_in)
+            n_rounds.append(n_in)
+            if r == 1:
+                nc.sync.dma_start(
+                    out=w_planes[:].rearrange("p i t c -> p (i t) c"),
+                    in_=w2.rearrange("i n (t p) c -> p (i n t) c", t=PACK, p=P),
+                )
+
+        ident_f32 = keep.tile([P, P], F32)
+        make_identity(nc, ident_f32[:])
+        ident_bf16 = keep.tile([P, P], BF16)
+        make_identity(nc, ident_bf16[:])
+        ones = keep.tile([P, P], BF16)
+        nc.vector.memset(ones[:], 1.0)
+
+        bias_sum_bank = psum.tile([P, CH], F32, tag="bank")
+        nc.tensor.matmul(out=bias_sum_bank[:], lhsT=ones[:], rhs=bias_rows[:], start=True, stop=True)
+        bias_sum = keep.tile([P, CH], F32)
+        nc.vector.tensor_copy(out=bias_sum[:], in_=bias_sum_bank[:])
+
+        bias_k_bank = psum.tile([P, PACK, P], BF16, tag="bank")
+        for t in range(PACK):
+            nc.tensor.transpose(bias_k_bank[:, t, :], bias_rows[:, t * P : (t + 1) * P], ident_bf16[:])
+        bias_k = keep.tile([P, PACK], F32)
+        nc.vector.tensor_copy(out=bias_k[:], in_=bias_k_bank[:, :, 0])
+
+        def combine(raw, op):
+            combined = stage.tile([P, PACK, CH], BF16)
+            nc.vector.tensor_tensor(out=combined[:], in0=raw[:, 0], in1=raw[:, 1], op=op)
+            return combined
+
+        def group(combined):
+            grouped = stage.tile([P, CH, PACK], BF16, align_bytes=64)
+            nc.vector.tensor_copy(
+                out=grouped[:].rearrange("p (c i) t -> p c t i", i=4),
+                in_=combined[:].rearrange("p t (c i) -> p c t i", i=4),
+            )
+            return grouped
+
+        def quantise(grouped, pool, width, name):
+            codes = pool.tile([P, width], U32, name=name + "_codes", align_bytes=64)
+            scales = pool.tile([P, width], U8, name=name + "_scales", align_bytes=64)
+            nc.vector.quantize_mx(
+                out=codes[:].bitcast(FP8X4),
+                scales=scales[:],
+                in_=grouped[:].rearrange("p w t -> p (w t)"),
+            )
+            return codes, scales
+
+        def multiply(bank, stationary, stationary_cols, moving, moving_cols, start, stop):
+            nc.tensor.matmul_mx(
+                out=bank,
+                lhsT=stationary[0][:, stationary_cols].bitcast(FP8X4),
+                lhsT_scale=stationary[1][:, stationary_cols],
+                rhs=moving[0][:, moving_cols].bitcast(FP8X4),
+                rhs_scale=moving[1][:, moving_cols],
+                start=start,
+                stop=stop,
+            )
+
+        def transpose_inputs(r):
+            banks = []
+            for x_in in (k_rounds[r], n_rounds[r]):
+                words = x_in[:].bitcast(F32)
+                for half in range(2):
+                    bank = psum.tile([P, 2, 2, P], F32, tag="bank")
+                    for l in range(2):
+                        for u in range(2):
+                            nc.tensor.transpose(
+                                bank[:, l, u, :],
+                                words[:, 2 * half + l, u * P : (u + 1) * P],
+                                ident_f32[:],
+                            )
+                    banks.append(bank)
+            return banks
+
+        def quantise_inputs(banks):
+            operands = []
+            for x, name in enumerate(("k", "n")):
+                grouped = stage.tile([P, ROUND, PACK], BF16, name=name + "_grouped", align_bytes=64)
+                words = grouped[:].bitcast(F32)
+                for half in range(2):
+                    nc.scalar.copy(
+                        out=words[:, half * 2 * P : (half + 1) * 2 * P, :].rearrange(
+                            "p (l r) u -> p l r u", l=2
+                        ),
+                        in_=banks[2 * x + half][:].rearrange("p l u r -> p l r u"),
+                    )
+                operands.append(quantise(grouped, quantised, ROUND, name))
+            return operands
+
+        def first_layer(k_q, n_q):
+            grouped = stage.tile([P, ROUND, PACK], BF16, name="o_grouped", align_bytes=64)
+            for j in range(ROUND_TILES):
+                tokens = slice(j * P, (j + 1) * P)
+                bank = psum.tile([P, PACK, P], F32, tag="bank")
+                for t in range(PACK):
+                    channels = slice(t * P, (t + 1) * P)
+                    multiply(bank[:, t, :], wa_pairs, channels, k_q, tokens, True, False)
+                    multiply(bank[:, t, :], wb_pairs, channels, n_q, tokens, False, True)
+                nc.vector.scalar_tensor_tensor(
+                    out=grouped[:, tokens, :],
+                    in0=bank[:].rearrange("p t r -> p r t"),
+                    scalar=0.5,
+                    in1=bias_k[:].unsqueeze(1).to_broadcast([P, P, PACK]),
+                    op0=ALU.mult,
+                    op1=ALU.add,
+                )
+            return quantise(grouped, quantised, ROUND, "o")
+
+        def second_layer(r, k_q, n_q, o_q):
+            everything = slice(0, CH)
+            for j in range(ROUND_TILES):
+                tokens = slice(j * P, (j + 1) * P)
+                bank = psum.tile([P, CH], F32, tag="bank")
+                multiply(bank[:], k_q, tokens, wa_pairs, everything, True, False)
+                multiply(bank[:], n_q, tokens, wb_pairs, everything, False, False)
+                multiply(bank[:], n_q, tokens, wa_pairs, everything, False, False)
+                multiply(bank[:], o_q, tokens, wb_planes, everything, False, True)
+                y = finish.tile([P, CH], F32)
+                nc.vector.scalar_tensor_tensor(
+                    out=y[:], in0=bank[:], scalar=0.5, in1=bias_sum[:], op0=ALU.mult, op1=ALU.add
+                )
+                above = finish.tile([P, CH], F32)
+                nc.scalar.activation(out=above[:], in_=y[:], func=ACT.Relu, bias=-THRESHOLD, scale=1.0)
+                below = finish.tile([P, CH], F32)
+                nc.scalar.activation(out=below[:], in_=y[:], func=ACT.Relu, bias=-THRESHOLD, scale=-1.0)
+                result = finish.tile([P, CH], F32)
+                nc.gpsimd.tensor_tensor(out=result[:], in0=above[:], in1=below[:], op=ALU.subtract)
+                nc.sync.dma_start(out=out_dram[:, r * ROUND_TILES + j, :], in_=result[:])
+
+        k_q = {}
+        n_q = {}
+        o_q = {}
+
+        banks = transpose_inputs(0)
+        wa_combined = combine(w_pairs, ALU.add)
+        wb_combined = combine(w_pairs, ALU.subtract)
+        wa_grouped = group(wa_combined)
+        wb_grouped = group(wb_combined)
+        wa_pairs = quantise(wa_grouped, keep, CH, "wa_pairs")
+        wb_pairs = quantise(wb_grouped, keep, CH, "wb_pairs")
+        k_q[0], n_q[0] = quantise_inputs(banks)
+
+        banks = transpose_inputs(1)
+        o_q[0] = first_layer(k_q[0], n_q[0])
+        k_q[1], n_q[1] = quantise_inputs(banks)
+        wb_planes = quantise(group(combine(w_planes, ALU.subtract)), keep, CH, "wb_planes")
+
+        for r in range(2, ROUNDS):
+            banks = transpose_inputs(r)
+            o_q[r - 1] = first_layer(k_q[r - 1], n_q[r - 1])
+            k_q[r], n_q[r] = quantise_inputs(banks)
+            second_layer(r - 2, k_q[r - 2], n_q[r - 2], o_q[r - 2])
+
+        o_q[ROUNDS - 1] = first_layer(k_q[ROUNDS - 1], n_q[ROUNDS - 1])
+        second_layer(ROUNDS - 2, k_q[ROUNDS - 2], n_q[ROUNDS - 2], o_q[ROUNDS - 2])
+        second_layer(ROUNDS - 1, k_q[ROUNDS - 1], n_q[ROUNDS - 1], o_q[ROUNDS - 1])

@@ -20,6 +20,7 @@ ROUND_TILES = 4
 ROUND = ROUND_TILES * P
 ROUNDS = TILES // ROUND_TILES
 THRESHOLD = 0.01
+RESULT_BUFS = 8
 
 FLOPS = 4 * 2 * TOKENS * CH * CH
 
@@ -60,7 +61,7 @@ def tile_afno2d_pb_t_kernel(tc, o1k, o1n, w2, b2, out):
             nc.sync.dma_start(out=n_in[:], in_=n_dram[:, tiles_of_round, :])
             k_rounds.append(k_in)
             n_rounds.append(n_in)
-            if r == 1:
+            if r == 0:
                 nc.sync.dma_start(
                     out=w_planes[:].rearrange("p i t c -> p (i t) c"),
                     in_=w2.rearrange("i n (t p) c -> p (i n t) c", t=PACK, p=P),
@@ -89,23 +90,25 @@ def tile_afno2d_pb_t_kernel(tc, o1k, o1n, w2, b2, out):
             nc.vector.tensor_tensor(out=combined[:], in0=raw[:, 0], in1=raw[:, 1], op=op)
             return combined
 
-        def group(combined):
+        def group(combined, copy):
             grouped = stage.tile([P, CH, PACK], BF16, align_bytes=64)
-            nc.vector.tensor_copy(
+            copy(
                 out=grouped[:].rearrange("p (c i) t -> p c t i", i=4),
                 in_=combined[:].rearrange("p t (c i) -> p c t i", i=4),
             )
             return grouped
 
-        def quantise(grouped, pool, width, name):
-            codes = pool.tile([P, width], U32, name=name + "_codes", align_bytes=64)
-            scales = pool.tile([P, width], U8, name=name + "_scales", align_bytes=64)
-            nc.vector.quantize_mx(
-                out=codes[:].bitcast(FP8X4),
-                scales=scales[:],
-                in_=grouped[:].rearrange("p w t -> p (w t)"),
-            )
+        def new_operand(pool, name):
+            codes = pool.tile([P, CH], U32, name=name + "_codes", align_bytes=64)
+            scales = pool.tile([P, CH], U8, name=name + "_scales", align_bytes=64)
             return codes, scales
+
+        def quantise(grouped, operand, cols):
+            nc.vector.quantize_mx(
+                out=operand[0][:, cols].bitcast(FP8X4),
+                scales=operand[1][:, cols],
+                in_=grouped[:, cols, :].rearrange("p w t -> p (w t)"),
+            )
 
         def multiply(bank, stationary, stationary_cols, moving, moving_cols, start, stop):
             nc.tensor.matmul_mx(
@@ -117,6 +120,17 @@ def tile_afno2d_pb_t_kernel(tc, o1k, o1n, w2, b2, out):
                 start=start,
                 stop=stop,
             )
+
+        everything = slice(0, CH)
+        wa_pairs = new_operand(keep, "wa_pairs")
+        wb_pairs = new_operand(keep, "wb_pairs")
+        wb_planes = new_operand(keep, "wb_planes")
+
+        x_grouped = {}
+        x_q = {}
+        o_grouped = {}
+        o_q = {}
+        y_tiles = {}
 
         def transpose_inputs(r):
             banks = []
@@ -132,87 +146,98 @@ def tile_afno2d_pb_t_kernel(tc, o1k, o1n, w2, b2, out):
                                 ident_f32[:],
                             )
                     banks.append(bank)
+            x_grouped[r] = (
+                stage.tile([P, ROUND, PACK], BF16, name="k_grouped", align_bytes=64),
+                stage.tile([P, ROUND, PACK], BF16, name="n_grouped", align_bytes=64),
+            )
+            x_q[r] = (new_operand(quantised, "k"), new_operand(quantised, "n"))
             return banks
 
-        def quantise_inputs(banks):
-            operands = []
-            for x, name in enumerate(("k", "n")):
-                grouped = stage.tile([P, ROUND, PACK], BF16, name=name + "_grouped", align_bytes=64)
-                words = grouped[:].bitcast(F32)
-                for half in range(2):
-                    nc.scalar.copy(
-                        out=words[:, half * 2 * P : (half + 1) * 2 * P, :].rearrange(
-                            "p (l r) u -> p l r u", l=2
-                        ),
-                        in_=banks[2 * x + half][:].rearrange("p l u r -> p l r u"),
-                    )
-                operands.append(quantise(grouped, quantised, ROUND, name))
-            return operands
+        def copy_out(r, b, bank):
+            words = x_grouped[r][b // 2][:].bitcast(F32)
+            half = b % 2
+            nc.scalar.copy(
+                out=words[:, half * 2 * P : (half + 1) * 2 * P, :].rearrange("p (l r) u -> p l r u", l=2),
+                in_=bank[:].rearrange("p l u r -> p l r u"),
+            )
 
-        def first_layer(k_q, n_q):
-            grouped = stage.tile([P, ROUND, PACK], BF16, name="o_grouped", align_bytes=64)
+        def quantise_input(r, b):
+            half = b % 2
+            quantise(x_grouped[r][b // 2], x_q[r][b // 2], slice(half * 2 * P, (half + 1) * 2 * P))
+
+        def first_layer(r, j):
+            if j == 0:
+                o_grouped[r] = stage.tile([P, ROUND, PACK], BF16, name="o_grouped", align_bytes=64)
+                o_q[r] = new_operand(quantised, "o")
+            k_q, n_q = x_q[r]
+            tokens = slice(j * P, (j + 1) * P)
+            bank = psum.tile([P, PACK, P], F32, tag="bank")
+            for t in range(PACK):
+                channels = slice(t * P, (t + 1) * P)
+                multiply(bank[:, t, :], wa_pairs, channels, k_q, tokens, True, False)
+                multiply(bank[:, t, :], wb_pairs, channels, n_q, tokens, False, True)
+            nc.vector.scalar_tensor_tensor(
+                out=o_grouped[r][:, tokens, :],
+                in0=bank[:].rearrange("p t r -> p r t"),
+                scalar=0.5,
+                in1=bias_k[:].unsqueeze(1).to_broadcast([P, P, PACK]),
+                op0=ALU.mult,
+                op1=ALU.add,
+            )
+
+        def second_layer(r, j):
+            k_q, n_q = x_q[r]
+            tokens = slice(j * P, (j + 1) * P)
+            bank = psum.tile([P, CH], F32, tag="bank")
+            multiply(bank[:], k_q, tokens, wa_pairs, everything, True, False)
+            multiply(bank[:], n_q, tokens, wb_pairs, everything, False, False)
+            multiply(bank[:], n_q, tokens, wa_pairs, everything, False, False)
+            multiply(bank[:], o_q[r], tokens, wb_planes, everything, False, True)
+            y = finish.tile([P, CH], F32)
+            nc.vector.scalar_tensor_tensor(
+                out=y[:], in0=bank[:], scalar=0.5, in1=bias_sum[:], op0=ALU.mult, op1=ALU.add
+            )
+            y_tiles[r * ROUND_TILES + j] = y
+
+        def softshrink_and_store(tile_index):
+            y = y_tiles[tile_index]
+            above = finish.tile([P, CH], F32)
+            nc.scalar.activation(out=above[:], in_=y[:], func=ACT.Relu, bias=-THRESHOLD, scale=1.0)
+            below = finish.tile([P, CH], F32)
+            nc.scalar.activation(out=below[:], in_=y[:], func=ACT.Relu, bias=-THRESHOLD, scale=-1.0)
+            result = finish.tile([P, CH], F32, bufs=RESULT_BUFS)
+            nc.gpsimd.tensor_tensor(out=result[:], in0=above[:], in1=below[:], op=ALU.subtract)
+            nc.sync.dma_start(out=out_dram[:, tile_index, :], in_=result[:])
+
+        def iteration(i):
+            transposing = i < ROUNDS
+            in_first_layer = 1 <= i <= ROUNDS
+            in_second_layer = i >= 2
+            if transposing:
+                banks = transpose_inputs(i)
             for j in range(ROUND_TILES):
-                tokens = slice(j * P, (j + 1) * P)
-                bank = psum.tile([P, PACK, P], F32, tag="bank")
-                for t in range(PACK):
-                    channels = slice(t * P, (t + 1) * P)
-                    multiply(bank[:, t, :], wa_pairs, channels, k_q, tokens, True, False)
-                    multiply(bank[:, t, :], wb_pairs, channels, n_q, tokens, False, True)
-                nc.vector.scalar_tensor_tensor(
-                    out=grouped[:, tokens, :],
-                    in0=bank[:].rearrange("p t r -> p r t"),
-                    scalar=0.5,
-                    in1=bias_k[:].unsqueeze(1).to_broadcast([P, P, PACK]),
-                    op0=ALU.mult,
-                    op1=ALU.add,
-                )
-            return quantise(grouped, quantised, ROUND, "o")
+                if transposing:
+                    copy_out(i, j, banks[j])
+                last_tile = (i - 2) * ROUND_TILES + j - 1
+                if last_tile >= 0:
+                    softshrink_and_store(last_tile)
+                if in_first_layer:
+                    first_layer(i - 1, j)
+                if transposing:
+                    quantise_input(i, j)
+                if in_first_layer:
+                    quantise(o_grouped[i - 1], o_q[i - 1], slice(j * P, (j + 1) * P))
+                if in_second_layer:
+                    second_layer(i - 2, j)
 
-        def second_layer(r, k_q, n_q, o_q):
-            everything = slice(0, CH)
-            for j in range(ROUND_TILES):
-                tokens = slice(j * P, (j + 1) * P)
-                bank = psum.tile([P, CH], F32, tag="bank")
-                multiply(bank[:], k_q, tokens, wa_pairs, everything, True, False)
-                multiply(bank[:], n_q, tokens, wb_pairs, everything, False, False)
-                multiply(bank[:], n_q, tokens, wa_pairs, everything, False, False)
-                multiply(bank[:], o_q, tokens, wb_planes, everything, False, True)
-                y = finish.tile([P, CH], F32)
-                nc.vector.scalar_tensor_tensor(
-                    out=y[:], in0=bank[:], scalar=0.5, in1=bias_sum[:], op0=ALU.mult, op1=ALU.add
-                )
-                above = finish.tile([P, CH], F32)
-                nc.scalar.activation(out=above[:], in_=y[:], func=ACT.Relu, bias=-THRESHOLD, scale=1.0)
-                below = finish.tile([P, CH], F32)
-                nc.scalar.activation(out=below[:], in_=y[:], func=ACT.Relu, bias=-THRESHOLD, scale=-1.0)
-                result = finish.tile([P, CH], F32)
-                nc.gpsimd.tensor_tensor(out=result[:], in0=above[:], in1=below[:], op=ALU.subtract)
-                nc.sync.dma_start(out=out_dram[:, r * ROUND_TILES + j, :], in_=result[:])
-
-        k_q = {}
-        n_q = {}
-        o_q = {}
-
-        banks = transpose_inputs(0)
         wa_combined = combine(w_pairs, ALU.add)
         wb_combined = combine(w_pairs, ALU.subtract)
-        wa_grouped = group(wa_combined)
-        wb_grouped = group(wb_combined)
-        wa_pairs = quantise(wa_grouped, keep, CH, "wa_pairs")
-        wb_pairs = quantise(wb_grouped, keep, CH, "wb_pairs")
-        k_q[0], n_q[0] = quantise_inputs(banks)
-
-        banks = transpose_inputs(1)
-        o_q[0] = first_layer(k_q[0], n_q[0])
-        k_q[1], n_q[1] = quantise_inputs(banks)
-        wb_planes = quantise(group(combine(w_planes, ALU.subtract)), keep, CH, "wb_planes")
-
-        for r in range(2, ROUNDS):
-            banks = transpose_inputs(r)
-            o_q[r - 1] = first_layer(k_q[r - 1], n_q[r - 1])
-            k_q[r], n_q[r] = quantise_inputs(banks)
-            second_layer(r - 2, k_q[r - 2], n_q[r - 2], o_q[r - 2])
-
-        o_q[ROUNDS - 1] = first_layer(k_q[ROUNDS - 1], n_q[ROUNDS - 1])
-        second_layer(ROUNDS - 2, k_q[ROUNDS - 2], n_q[ROUNDS - 2], o_q[ROUNDS - 2])
-        second_layer(ROUNDS - 1, k_q[ROUNDS - 1], n_q[ROUNDS - 1], o_q[ROUNDS - 1])
+        wa_grouped = group(wa_combined, nc.scalar.copy)
+        wb_grouped = group(wb_combined, nc.vector.tensor_copy)
+        quantise(wb_grouped, wb_pairs, everything)
+        quantise(wa_grouped, wa_pairs, everything)
+        iteration(0)
+        quantise(group(combine(w_planes, ALU.subtract), nc.vector.tensor_copy), wb_planes, everything)
+        for i in range(1, ROUNDS + 2):
+            iteration(i)
+        softshrink_and_store(TILES - 1)

@@ -14,13 +14,13 @@ ACT = mybir.ActivationFunctionType
 P = 128
 PACK = 4
 CH = P * PACK
+HALF = CH // 2
 TOKENS = 64 * 64
 TILES = TOKENS // P
 ROUND_TILES = 4
 ROUND = ROUND_TILES * P
 ROUNDS = TILES // ROUND_TILES
 THRESHOLD = 0.01
-RESULT_BUFS = 8
 
 FLOPS = 4 * 2 * TOKENS * CH * CH
 
@@ -32,8 +32,8 @@ def tile_afno2d_pb_t_kernel(tc, o1k, o1n, w2, b2, out):
         keep = ctx.enter_context(tc.tile_pool(name="keep", bufs=1))
         inputs = ctx.enter_context(tc.tile_pool(name="inputs", bufs=ROUNDS))
         stage = ctx.enter_context(tc.tile_pool(name="stage", bufs=2))
-        quantised = ctx.enter_context(tc.tile_pool(name="quantised", bufs=4))
-        finish = ctx.enter_context(tc.tile_pool(name="finish", bufs=4))
+        quantised = ctx.enter_context(tc.tile_pool(name="quantised", bufs=3))
+        finish = ctx.enter_context(tc.tile_pool(name="finish", bufs=8))
         psum = ctx.enter_context(tc.psum_pool(name="psum", bufs=8))
 
         k_dram = o1k.rearrange("b h w n c -> (b h w n) c").rearrange("(p j) c -> p j c", j=TILES)
@@ -42,14 +42,13 @@ def tile_afno2d_pb_t_kernel(tc, o1k, o1n, w2, b2, out):
 
         bias_rows = keep.tile([P, CH], BF16)
         nc.vector.memset(bias_rows[:], 0.0)
-        nc.sync.dma_start(out=bias_rows[0:2, :], in_=b2.rearrange("i n c -> (i n) c"))
 
-        w_pairs = keep.tile([P, 2, PACK, CH], BF16)
+        w_raw = keep.tile([P, 2, PACK, CH], BF16)
         nc.sync.dma_start(
-            out=w_pairs[:].rearrange("p i (u e) c -> p (i u) (e c)", e=2),
+            out=w_raw[:].rearrange("p i (u e) c -> p (i u) (e c)", e=2),
             in_=w2.rearrange("i n (u p e) c -> p (i n u) (e c)", u=2, p=P, e=2),
         )
-        w_planes = keep.tile([P, 2, PACK, CH], BF16)
+        nc.sync.dma_start(out=bias_rows[0:2, :], in_=b2.rearrange("i n c -> (i n) c"))
 
         k_rounds = []
         n_rounds = []
@@ -61,42 +60,28 @@ def tile_afno2d_pb_t_kernel(tc, o1k, o1n, w2, b2, out):
             nc.sync.dma_start(out=n_in[:], in_=n_dram[:, tiles_of_round, :])
             k_rounds.append(k_in)
             n_rounds.append(n_in)
-            if r == 0:
-                nc.sync.dma_start(
-                    out=w_planes[:].rearrange("p i t c -> p (i t) c"),
-                    in_=w2.rearrange("i n (t p) c -> p (i n t) c", t=PACK, p=P),
-                )
 
         ident_f32 = keep.tile([P, P], F32)
         make_identity(nc, ident_f32[:])
-        ident_bf16 = keep.tile([P, P], BF16)
-        make_identity(nc, ident_bf16[:])
         ones = keep.tile([P, P], BF16)
         nc.vector.memset(ones[:], 1.0)
+        bias_neg = keep.tile([P, CH], F32)
+        bias_k = keep.tile([P, 2, 2], F32)
 
-        bias_sum_bank = psum.tile([P, CH], F32, tag="bank")
-        nc.tensor.matmul(out=bias_sum_bank[:], lhsT=ones[:], rhs=bias_rows[:], start=True, stop=True)
-        bias_sum = keep.tile([P, CH], F32)
-        nc.vector.tensor_copy(out=bias_sum[:], in_=bias_sum_bank[:])
-
-        bias_k_bank = psum.tile([P, PACK, P], BF16, tag="bank")
-        for t in range(PACK):
-            nc.tensor.transpose(bias_k_bank[:, t, :], bias_rows[:, t * P : (t + 1) * P], ident_bf16[:])
-        bias_k = keep.tile([P, PACK], F32)
-        nc.vector.tensor_copy(out=bias_k[:], in_=bias_k_bank[:, :, 0])
-
-        def combine(raw, op):
-            combined = stage.tile([P, PACK, CH], BF16)
-            nc.vector.tensor_tensor(out=combined[:], in0=raw[:, 0], in1=raw[:, 1], op=op)
-            return combined
-
-        def group(combined, copy):
-            grouped = stage.tile([P, CH, PACK], BF16, align_bytes=64)
-            copy(
-                out=grouped[:].rearrange("p (c i) t -> p c t i", i=4),
-                in_=combined[:].rearrange("p t (c i) -> p c t i", i=4),
+        def prepare_biases():
+            sum_bank = psum.tile([P, CH], F32, tag="bank")
+            nc.tensor.matmul(out=sum_bank[:], lhsT=ones[:], rhs=bias_rows[:], start=True, stop=True)
+            words_bank = psum.tile([P, 2, P], F32, tag="bank")
+            words = bias_rows[:].bitcast(F32)
+            for u in range(2):
+                nc.tensor.transpose(words_bank[:, u, :], words[:, u * P : (u + 1) * P], ident_f32[:])
+            nc.vector.tensor_scalar(
+                out=bias_neg[:], in0=sum_bank[:], scalar1=-1.0, scalar2=THRESHOLD, op0=ALU.mult, op1=ALU.add
             )
-            return grouped
+            pairs = words_bank[:].rearrange("p u r -> p (u r)").bitcast(BF16)
+            nc.vector.tensor_copy(
+                out=bias_k[:], in_=pairs.rearrange("p (u x) -> p u x", u=2)[:, :, 0:2]
+            )
 
         def new_operand(pool, name):
             codes = pool.tile([P, CH], U32, name=name + "_codes", align_bytes=64)
@@ -122,15 +107,40 @@ def tile_afno2d_pb_t_kernel(tc, o1k, o1n, w2, b2, out):
             )
 
         everything = slice(0, CH)
-        wa_pairs = new_operand(keep, "wa_pairs")
-        wb_pairs = new_operand(keep, "wb_pairs")
-        wb_planes = new_operand(keep, "wb_planes")
+        halves = (slice(0, HALF), slice(HALF, CH))
+        wa = new_operand(keep, "wa")
+        wb = new_operand(keep, "wb")
+        combined_wa = keep.tile([P, PACK, CH], BF16)
+        combined_wb = keep.tile([P, PACK, CH], BF16)
+        grouped_wa = keep.tile([P, CH, PACK], BF16, align_bytes=64)
+        grouped_wb = keep.tile([P, CH, PACK], BF16, align_bytes=64)
+
+        def combine(combined, op, u):
+            nc.vector.tensor_tensor(
+                out=combined[:, :, halves[u]],
+                in0=w_raw[:, 0, :, halves[u]],
+                in1=w_raw[:, 1, :, halves[u]],
+                op=op,
+            )
+
+        def group(grouped, combined, u, copy):
+            copy(
+                out=grouped[:].rearrange("p (e x) t -> p e x t", e=2)[:, :, u * P : (u + 1) * P, :],
+                in_=combined[:, :, halves[u]].rearrange("p t (m e) -> p e m t", e=2),
+            )
+
+        def quantise_weight(grouped, operand, u):
+            for e in range(2):
+                start = e * HALF + u * P
+                quantise(grouped, operand, slice(start, start + P))
 
         x_grouped = {}
         x_q = {}
+        planes = {}
         o_grouped = {}
         o_q = {}
-        y_tiles = {}
+        shifted = {}
+        positive = {}
 
         def transpose_inputs(r):
             banks = []
@@ -161,83 +171,142 @@ def tile_afno2d_pb_t_kernel(tc, o1k, o1n, w2, b2, out):
                 in_=bank[:].rearrange("p l u r -> p l r u"),
             )
 
-        def quantise_input(r, b):
-            half = b % 2
-            quantise(x_grouped[r][b // 2], x_q[r][b // 2], slice(half * 2 * P, (half + 1) * 2 * P))
+        def quantise_input(r, which):
+            quantise(x_grouped[r][which], x_q[r][which], everything)
 
-        def first_layer(r, j):
-            if j == 0:
+        def first_layer(r, t):
+            if t == 0:
+                planes[r] = stage.tile([P, PACK, ROUND], BF16, name="planes")
                 o_grouped[r] = stage.tile([P, ROUND, PACK], BF16, name="o_grouped", align_bytes=64)
                 o_q[r] = new_operand(quantised, "o")
             k_q, n_q = x_q[r]
-            tokens = slice(j * P, (j + 1) * P)
-            bank = psum.tile([P, PACK, P], F32, tag="bank")
-            for t in range(PACK):
-                channels = slice(t * P, (t + 1) * P)
-                multiply(bank[:, t, :], wa_pairs, channels, k_q, tokens, True, False)
-                multiply(bank[:, t, :], wb_pairs, channels, n_q, tokens, False, True)
-            nc.vector.scalar_tensor_tensor(
-                out=o_grouped[r][:, tokens, :],
-                in0=bank[:].rearrange("p t r -> p r t"),
-                scalar=0.5,
-                in1=bias_k[:].unsqueeze(1).to_broadcast([P, P, PACK]),
-                op0=ALU.mult,
-                op1=ALU.add,
+            start = (t % 2) * HALF + (t // 2) * P
+            channels = slice(start, start + P)
+            bank = psum.tile([P, ROUND], F32, tag="bank")
+            multiply(bank[:], wa, channels, k_q, everything, True, False)
+            multiply(bank[:], wb, channels, n_q, everything, False, True)
+            return bank
+
+        def add_bias(r, t, bank):
+            nc.scalar.activation(
+                out=planes[r][:, t, :],
+                in_=bank[:],
+                func=ACT.Identity,
+                bias=bias_k[:, t // 2, t % 2 : t % 2 + 1],
+                scale=0.5,
             )
+
+        def interleave(r, h):
+            nc.vector.tensor_copy(
+                out=o_grouped[r][:, halves[h], :].rearrange("p (c i) t -> p c t i", i=4),
+                in_=planes[r][:, :, halves[h]].rearrange("p t (c i) -> p c t i", i=4),
+            )
+
+        def quantise_o(r, h):
+            quantise(o_grouped[r], o_q[r], halves[h])
 
         def second_layer(r, j):
             k_q, n_q = x_q[r]
             tokens = slice(j * P, (j + 1) * P)
             bank = psum.tile([P, CH], F32, tag="bank")
-            multiply(bank[:], k_q, tokens, wa_pairs, everything, True, False)
-            multiply(bank[:], n_q, tokens, wb_pairs, everything, False, False)
-            multiply(bank[:], n_q, tokens, wa_pairs, everything, False, False)
-            multiply(bank[:], o_q[r], tokens, wb_planes, everything, False, True)
-            y = finish.tile([P, CH], F32)
-            nc.vector.scalar_tensor_tensor(
-                out=y[:], in0=bank[:], scalar=0.5, in1=bias_sum[:], op0=ALU.mult, op1=ALU.add
-            )
-            y_tiles[r * ROUND_TILES + j] = y
+            multiply(bank[:], k_q, tokens, wa, everything, True, False)
+            multiply(bank[:], n_q, tokens, wb, everything, False, False)
+            multiply(bank[:], n_q, tokens, wa, everything, False, False)
+            multiply(bank[:], o_q[r], tokens, wb, everything, False, True)
+            return bank
 
-        def softshrink_and_store(tile_index):
-            y = y_tiles[tile_index]
-            above = finish.tile([P, CH], F32)
-            nc.scalar.activation(out=above[:], in_=y[:], func=ACT.Relu, bias=-THRESHOLD, scale=1.0)
-            below = finish.tile([P, CH], F32)
-            nc.scalar.activation(out=below[:], in_=y[:], func=ACT.Relu, bias=-THRESHOLD, scale=-1.0)
-            result = finish.tile([P, CH], F32, bufs=RESULT_BUFS)
-            nc.gpsimd.tensor_tensor(out=result[:], in0=above[:], in1=below[:], op=ALU.subtract)
-            nc.sync.dma_start(out=out_dram[:, tile_index, :], in_=result[:])
+        def leave(n, bank):
+            w = finish.tile([P, CH], F32, name="shifted")
+            nc.vector.scalar_tensor_tensor(
+                out=w[:].rearrange("p (x e) -> p x e", e=2),
+                in0=bank[:].rearrange("p (e x) -> p x e", e=2),
+                scalar=-0.5,
+                in1=bias_neg[:].rearrange("p (x e) -> p x e", e=2),
+                op0=ALU.mult,
+                op1=ALU.add,
+            )
+            shifted[n] = w
+
+        def relu(n):
+            a = finish.tile([P, CH], F32, name="positive")
+            nc.scalar.activation(out=a[:], in_=shifted[n][:], func=ACT.Relu)
+            positive[n] = a
+
+        def finish_tile(n):
+            result = finish.tile([P, CH], F32, name="result")
+            nc.vector.scalar_tensor_tensor(
+                out=result[:],
+                in0=positive[n][:],
+                scalar=2.0 * THRESHOLD,
+                in1=shifted[n][:],
+                op0=ALU.min,
+                op1=ALU.subtract,
+            )
+            nc.sync.dma_start(out=out_dram[:, n, :], in_=result[:])
 
         def iteration(i):
             transposing = i < ROUNDS
-            in_first_layer = 1 <= i <= ROUNDS
-            in_second_layer = i >= 2
+            in_first = 1 <= i <= ROUNDS
+            in_second = i >= 2
+            before = (i - 3) * ROUND_TILES
+            here = (i - 2) * ROUND_TILES
             if transposing:
                 banks = transpose_inputs(i)
-            for j in range(ROUND_TILES):
-                if transposing:
-                    copy_out(i, j, banks[j])
-                last_tile = (i - 2) * ROUND_TILES + j - 1
-                if last_tile >= 0:
-                    softshrink_and_store(last_tile)
-                if in_first_layer:
-                    first_layer(i - 1, j)
-                if transposing:
-                    quantise_input(i, j)
-                if in_first_layer:
-                    quantise(o_grouped[i - 1], o_q[i - 1], slice(j * P, (j + 1) * P))
-                if in_second_layer:
-                    second_layer(i - 2, j)
+            if before >= 0:
+                relu(before + 3)
+            if transposing:
+                copy_out(i, 0, banks[0])
+                copy_out(i, 1, banks[1])
+            if before >= 0:
+                finish_tile(before)
+                finish_tile(before + 1)
+            if transposing:
+                quantise_input(i, 0)
+                copy_out(i, 2, banks[2])
+                copy_out(i, 3, banks[3])
+            if before >= 0:
+                finish_tile(before + 2)
+                finish_tile(before + 3)
+            if in_first:
+                for t in range(PACK):
+                    add_bias(i - 1, t, first_layer(i - 1, t))
+            if transposing:
+                quantise_input(i, 1)
+            if in_second:
+                leave(here, second_layer(i - 2, 0))
+                relu(here)
+            if in_first:
+                interleave(i - 1, 0)
+            if in_second:
+                leave(here + 1, second_layer(i - 2, 1))
+                relu(here + 1)
+            if in_first:
+                interleave(i - 1, 1)
+                quantise_o(i - 1, 0)
+            if in_second:
+                leave(here + 2, second_layer(i - 2, 2))
+                relu(here + 2)
+            if in_first:
+                quantise_o(i - 1, 1)
+            if in_second:
+                leave(here + 3, second_layer(i - 2, 3))
 
-        wa_combined = combine(w_pairs, ALU.add)
-        wb_combined = combine(w_pairs, ALU.subtract)
-        wa_grouped = group(wa_combined, nc.scalar.copy)
-        wb_grouped = group(wb_combined, nc.vector.tensor_copy)
-        quantise(wb_grouped, wb_pairs, everything)
-        quantise(wa_grouped, wa_pairs, everything)
-        iteration(0)
-        quantise(group(combine(w_planes, ALU.subtract), nc.vector.tensor_copy), wb_planes, everything)
-        for i in range(1, ROUNDS + 2):
+        combine(combined_wa, ALU.add, 0)
+        group(grouped_wa, combined_wa, 0, nc.scalar.copy)
+        combine(combined_wb, ALU.subtract, 0)
+        combine(combined_wa, ALU.add, 1)
+        group(grouped_wa, combined_wa, 1, nc.scalar.copy)
+        group(grouped_wb, combined_wb, 0, nc.vector.tensor_copy)
+        combine(combined_wb, ALU.subtract, 1)
+        quantise_weight(grouped_wb, wb, 0)
+        quantise_weight(grouped_wa, wa, 0)
+        group(grouped_wb, combined_wb, 1, nc.vector.tensor_copy)
+        prepare_biases()
+        quantise_weight(grouped_wb, wb, 1)
+        quantise_weight(grouped_wa, wa, 1)
+        for i in range(ROUNDS + 2):
             iteration(i)
-        softshrink_and_store(TILES - 1)
+        last = (ROUNDS - 1) * ROUND_TILES
+        relu(last + 3)
+        for j in range(ROUND_TILES):
+            finish_tile(last + j)

@@ -17,9 +17,10 @@ CH = P * PACK
 HALF = CH // 2
 TOKENS = 64 * 64
 TILES = TOKENS // P
-ROUND_TILES = 4
-ROUND = ROUND_TILES * P
-ROUNDS = TILES // ROUND_TILES
+SIZES = (4,) * 8
+ROUNDS = len(SIZES)
+FIRST = tuple(sum(SIZES[:r]) for r in range(ROUNDS))
+WIDEST = max(SIZES) * P
 THRESHOLD = 0.01
 
 FLOPS = 4 * 2 * TOKENS * CH * CH
@@ -30,7 +31,7 @@ def tile_afno2d_pb_t_kernel(tc, o1k, o1n, w2, b2, out):
     with ExitStack() as ctx:
         ctx.enter_context(tc.manual_schedule())
         keep = ctx.enter_context(tc.tile_pool(name="keep", bufs=1))
-        inputs = ctx.enter_context(tc.tile_pool(name="inputs", bufs=ROUNDS))
+        inputs = ctx.enter_context(tc.tile_pool(name="inputs", bufs=1))
         stage = ctx.enter_context(tc.tile_pool(name="stage", bufs=2))
         quantised = ctx.enter_context(tc.tile_pool(name="quantised", bufs=3))
         finish = ctx.enter_context(tc.tile_pool(name="finish", bufs=8))
@@ -53,10 +54,10 @@ def tile_afno2d_pb_t_kernel(tc, o1k, o1n, w2, b2, out):
         k_rounds = []
         n_rounds = []
         for r in range(ROUNDS):
-            tiles_of_round = slice(r * ROUND_TILES, (r + 1) * ROUND_TILES)
-            k_in = inputs.tile([P, ROUND_TILES, CH], BF16)
+            tiles_of_round = slice(FIRST[r], FIRST[r] + SIZES[r])
+            k_in = inputs.tile([P, SIZES[r], CH], BF16, name="k_in%d" % r)
             nc.sync.dma_start(out=k_in[:], in_=k_dram[:, tiles_of_round, :])
-            n_in = inputs.tile([P, ROUND_TILES, CH], BF16)
+            n_in = inputs.tile([P, SIZES[r], CH], BF16, name="n_in%d" % r)
             nc.sync.dma_start(out=n_in[:], in_=n_dram[:, tiles_of_round, :])
             k_rounds.append(k_in)
             n_rounds.append(n_in)
@@ -142,68 +143,72 @@ def tile_afno2d_pb_t_kernel(tc, o1k, o1n, w2, b2, out):
         shifted = {}
         positive = {}
 
-        def transpose_inputs(r):
-            banks = []
-            for x_in in (k_rounds[r], n_rounds[r]):
-                words = x_in[:].bitcast(F32)
-                for half in range(2):
-                    bank = psum.tile([P, 2, 2, P], F32, tag="bank")
-                    for l in range(2):
-                        for u in range(2):
-                            nc.tensor.transpose(
-                                bank[:, l, u, :],
-                                words[:, 2 * half + l, u * P : (u + 1) * P],
-                                ident_f32[:],
-                            )
-                    banks.append(bank)
+        def start_round(r):
             x_grouped[r] = (
-                stage.tile([P, ROUND, PACK], BF16, name="k_grouped", align_bytes=64),
-                stage.tile([P, ROUND, PACK], BF16, name="n_grouped", align_bytes=64),
+                stage.tile([P, WIDEST, PACK], BF16, name="k_grouped", align_bytes=64),
+                stage.tile([P, WIDEST, PACK], BF16, name="n_grouped", align_bytes=64),
             )
             x_q[r] = (new_operand(quantised, "k"), new_operand(quantised, "n"))
-            return banks
 
-        def copy_out(r, b, bank):
-            words = x_grouped[r][b // 2][:].bitcast(F32)
-            half = b % 2
+        def transpose_input(r, which):
+            words = (k_rounds, n_rounds)[which][r][:].bitcast(F32)
+            for first in range(0, SIZES[r], 2):
+                here = min(2, SIZES[r] - first)
+                bank = psum.tile([P, 2, 2, P], F32, tag="bank")
+                for l in range(here):
+                    for u in range(2):
+                        nc.tensor.transpose(
+                            bank[:, l, u, :],
+                            words[:, first + l, u * P : (u + 1) * P],
+                            ident_f32[:],
+                        )
+                copy_out(r, which, first, here, bank)
+
+        def copy_out(r, which, first, here, bank):
+            words = x_grouped[r][which][:].rearrange("p r t -> p (r t)").bitcast(F32)
             nc.scalar.copy(
-                out=words[:, half * 2 * P : (half + 1) * 2 * P, :].rearrange("p (l r) u -> p l r u", l=2),
-                in_=bank[:].rearrange("p l u r -> p l r u"),
+                out=words[:, first * 2 * P : (first + here) * 2 * P].rearrange("p (l r u) -> p l r u", l=here, u=2),
+                in_=bank[:, 0:here].rearrange("p l u r -> p l r u"),
             )
 
         def quantise_input(r, which):
-            quantise(x_grouped[r][which], x_q[r][which], everything)
+            quantise(x_grouped[r][which], x_q[r][which], slice(0, SIZES[r] * P))
 
         def first_layer(r, t):
             if t == 0:
-                planes[r] = stage.tile([P, PACK, ROUND], BF16, name="planes")
-                o_grouped[r] = stage.tile([P, ROUND, PACK], BF16, name="o_grouped", align_bytes=64)
+                planes[r] = stage.tile([P, PACK, WIDEST], BF16, name="planes")
+                o_grouped[r] = stage.tile([P, WIDEST, PACK], BF16, name="o_grouped", align_bytes=64)
                 o_q[r] = new_operand(quantised, "o")
             k_q, n_q = x_q[r]
             start = (t % 2) * HALF + (t // 2) * P
             channels = slice(start, start + P)
-            bank = psum.tile([P, ROUND], F32, tag="bank")
-            multiply(bank[:], wa, channels, k_q, everything, True, False)
-            multiply(bank[:], wb, channels, n_q, everything, False, True)
+            bank = psum.tile([P, WIDEST], F32, tag="bank")
+            tokens = slice(0, SIZES[r] * P)
+            multiply(bank[:, tokens], wa, channels, k_q, tokens, True, False)
+            multiply(bank[:, tokens], wb, channels, n_q, tokens, False, True)
             return bank
 
         def add_bias(r, t, bank):
             nc.scalar.activation(
-                out=planes[r][:, t, :],
-                in_=bank[:],
+                out=planes[r][:, t, 0 : SIZES[r] * P],
+                in_=bank[:, 0 : SIZES[r] * P],
                 func=ACT.Identity,
                 bias=bias_k[:, t // 2, t % 2 : t % 2 + 1],
                 scale=0.5,
             )
 
-        def interleave(r, h):
-            nc.vector.tensor_copy(
-                out=o_grouped[r][:, halves[h], :].rearrange("p (c i) t -> p c t i", i=4),
-                in_=planes[r][:, :, halves[h]].rearrange("p t (c i) -> p c t i", i=4),
+        def interleave(r, cols, copy):
+            copy(
+                out=o_grouped[r][:, cols, :].rearrange("p (c i) t -> p c t i", i=4),
+                in_=planes[r][:, :, cols].rearrange("p t (c i) -> p c t i", i=4),
             )
 
         def quantise_o(r, h):
-            quantise(o_grouped[r], o_q[r], halves[h])
+            quantise(o_grouped[r], o_q[r], half_of(r, h))
+
+        def half_of(r, h):
+            width = SIZES[r] * P // 2
+            return slice(h * width, (h + 1) * width)
 
         def second_layer(r, j):
             k_q, n_q = x_q[r]
@@ -244,52 +249,60 @@ def tile_afno2d_pb_t_kernel(tc, o1k, o1n, w2, b2, out):
             )
             nc.sync.dma_start(out=out_dram[:, n, :], in_=result[:])
 
+        pending = []
+
+        def finish_one():
+            if pending:
+                finish_tile(pending.pop(0))
+
+        def half_steps(r):
+            a, b = half_of(r, 0), half_of(r, 1)
+            return [
+                lambda: interleave(r, a, nc.vector.tensor_copy),
+                lambda: interleave(r, b, nc.vector.tensor_copy),
+                lambda: quantise_o(r, 0),
+                lambda: quantise_o(r, 1),
+            ]
+
         def iteration(i):
             transposing = i < ROUNDS
             in_first = 1 <= i <= ROUNDS
             in_second = i >= 2
-            before = (i - 3) * ROUND_TILES
-            here = (i - 2) * ROUND_TILES
             if transposing:
-                banks = transpose_inputs(i)
-            if before >= 0:
-                relu(before + 3)
-            if transposing:
-                copy_out(i, 0, banks[0])
-                copy_out(i, 1, banks[1])
-            if before >= 0:
-                finish_tile(before)
-                finish_tile(before + 1)
+                start_round(i)
+                transpose_input(i, 0)
+            if pending:
+                relu(pending[-1])
+            while len(pending) > 1:
+                finish_one()
             if transposing:
                 quantise_input(i, 0)
-                copy_out(i, 2, banks[2])
-                copy_out(i, 3, banks[3])
-            if before >= 0:
-                finish_tile(before + 2)
-                finish_tile(before + 3)
+            finish_one()
+            steps = []
             if in_first:
                 for t in range(PACK):
                     add_bias(i - 1, t, first_layer(i - 1, t))
-            if transposing:
+                steps = half_steps(i - 1)
+            z = SIZES[i - 2] if in_second else 0
+            for j in range(z):
+                n = FIRST[i - 2] + j
+                if j == z // 2 and transposing:
+                    transpose_input(i, 1)
+                if j == z - 1 and transposing:
+                    quantise_input(i, 1)
+                leave(n, second_layer(i - 2, j))
+                if j < z - 1:
+                    relu(n)
+                if steps:
+                    steps.pop(0)()
+                if j >= z // 2 or not transposing:
+                    finish_one()
+                pending.append(n)
+            for step in steps:
+                step()
+            if transposing and z == 0:
+                transpose_input(i, 1)
                 quantise_input(i, 1)
-            if in_second:
-                leave(here, second_layer(i - 2, 0))
-                relu(here)
-            if in_first:
-                interleave(i - 1, 0)
-            if in_second:
-                leave(here + 1, second_layer(i - 2, 1))
-                relu(here + 1)
-            if in_first:
-                interleave(i - 1, 1)
-                quantise_o(i - 1, 0)
-            if in_second:
-                leave(here + 2, second_layer(i - 2, 2))
-                relu(here + 2)
-            if in_first:
-                quantise_o(i - 1, 1)
-            if in_second:
-                leave(here + 3, second_layer(i - 2, 3))
 
         combine(combined_wa, ALU.add, 0)
         group(grouped_wa, combined_wa, 0, nc.scalar.copy)
@@ -306,7 +319,6 @@ def tile_afno2d_pb_t_kernel(tc, o1k, o1n, w2, b2, out):
         quantise_weight(grouped_wa, wa, 1)
         for i in range(ROUNDS + 2):
             iteration(i)
-        last = (ROUNDS - 1) * ROUND_TILES
-        relu(last + 3)
-        for j in range(ROUND_TILES):
-            finish_tile(last + j)
+        relu(pending[-1])
+        while pending:
+            finish_one()

@@ -17,10 +17,29 @@ CH = P * PACK
 HALF = CH // 2
 TOKENS = 64 * 64
 TILES = TOKENS // P
-SIZES = (4,) * 8
+SIZES = (4,)*8
 ROUNDS = len(SIZES)
 FIRST = tuple(sum(SIZES[:r]) for r in range(ROUNDS))
 WIDEST = max(SIZES) * P
+S_COLS = 128
+XK = (1, 3)
+XN = (1, 3)
+CK = (1, 3)
+CN = (1, 3)
+QLAG = 1
+WARM = 0
+VX = ((1, 1, 0), (1, 1, 1))
+BIAS3 = True
+OQ = 2
+SQ = (2,)
+GFIRST = 22
+GMOD = 2
+SPLIT = True
+NPOS = 0
+QPOS = 2
+MERGE = False
+KQPOS = 1
+FPOS = 2
 THRESHOLD = 0.01
 
 FLOPS = 4 * 2 * TOKENS * CH * CH
@@ -32,9 +51,9 @@ def tile_afno2d_pb_t_kernel(tc, o1k, o1n, w2, b2, out):
         ctx.enter_context(tc.manual_schedule())
         keep = ctx.enter_context(tc.tile_pool(name="keep", bufs=1))
         inputs = ctx.enter_context(tc.tile_pool(name="inputs", bufs=1))
-        stage = ctx.enter_context(tc.tile_pool(name="stage", bufs=2))
-        quantised = ctx.enter_context(tc.tile_pool(name="quantised", bufs=3))
-        finish = ctx.enter_context(tc.tile_pool(name="finish", bufs=8))
+        stage = ctx.enter_context(tc.tile_pool(name="stage", bufs=3))
+        quantised = ctx.enter_context(tc.tile_pool(name="quantised", bufs=5))
+        finish = ctx.enter_context(tc.tile_pool(name="finish", bufs=4))
         psum = ctx.enter_context(tc.psum_pool(name="psum", bufs=8))
 
         k_dram = o1k.rearrange("b h w n c -> (b h w n) c").rearrange("(p j) c -> p j c", j=TILES)
@@ -43,13 +62,13 @@ def tile_afno2d_pb_t_kernel(tc, o1k, o1n, w2, b2, out):
 
         bias_rows = keep.tile([P, CH], BF16)
         nc.vector.memset(bias_rows[:], 0.0)
+        nc.sync.dma_start(out=bias_rows[0:2, :], in_=b2.rearrange("i n c -> (i n) c"))
 
         w_raw = keep.tile([P, 2, PACK, CH], BF16)
         nc.sync.dma_start(
             out=w_raw[:].rearrange("p i (u e) c -> p (i u) (e c)", e=2),
             in_=w2.rearrange("i n (u p e) c -> p (i n u) (e c)", u=2, p=P, e=2),
         )
-        nc.sync.dma_start(out=bias_rows[0:2, :], in_=b2.rearrange("i n c -> (i n) c"))
 
         k_rounds = []
         n_rounds = []
@@ -76,8 +95,8 @@ def tile_afno2d_pb_t_kernel(tc, o1k, o1n, w2, b2, out):
             words = bias_rows[:].bitcast(F32)
             for u in range(2):
                 nc.tensor.transpose(words_bank[:, u, :], words[:, u * P : (u + 1) * P], ident_f32[:])
-            nc.vector.tensor_scalar(
-                out=bias_neg[:], in0=sum_bank[:], scalar1=-1.0, scalar2=THRESHOLD, op0=ALU.mult, op1=ALU.add
+            nc.scalar.activation(
+                out=bias_neg[:], in_=sum_bank[:], func=ACT.Identity, bias=THRESHOLD, scale=-1.0
             )
             pairs = words_bank[:].rearrange("p u r -> p (u r)").bitcast(BF16)
             nc.vector.tensor_copy(
@@ -151,6 +170,8 @@ def tile_afno2d_pb_t_kernel(tc, o1k, o1n, w2, b2, out):
             x_q[r] = (new_operand(quantised, "k"), new_operand(quantised, "n"))
 
         def transpose_input(r, which):
+            if which == 0:
+                start_round(r)
             words = (k_rounds, n_rounds)[which][r][:].bitcast(F32)
             for first in range(0, SIZES[r], 2):
                 here = min(2, SIZES[r] - first)
@@ -162,17 +183,21 @@ def tile_afno2d_pb_t_kernel(tc, o1k, o1n, w2, b2, out):
                             words[:, first + l, u * P : (u + 1) * P],
                             ident_f32[:],
                         )
-                copy_out(r, which, first, here, bank)
+                x_banks[r, which, first // 2] = (first, here, bank)
 
         def copy_out(r, which, first, here, bank):
             words = x_grouped[r][which][:].rearrange("p r t -> p (r t)").bitcast(F32)
-            nc.scalar.copy(
+            copy = nc.vector.tensor_copy if (r, which, first // 2) in VX else nc.scalar.copy
+            copy(
                 out=words[:, first * 2 * P : (first + here) * 2 * P].rearrange("p (l r u) -> p l r u", l=here, u=2),
                 in_=bank[:, 0:here].rearrange("p l u r -> p l r u"),
             )
 
         def quantise_input(r, which):
             quantise(x_grouped[r][which], x_q[r][which], slice(0, SIZES[r] * P))
+
+        def quantise_input_part(r, which, half):
+            quantise(x_grouped[r][which], x_q[r][which], slice(half * 2 * P, min((half + 1) * 2, SIZES[r]) * P))
 
         def first_layer(r, t):
             if t == 0:
@@ -222,103 +247,184 @@ def tile_afno2d_pb_t_kernel(tc, o1k, o1n, w2, b2, out):
 
         def leave(n, bank):
             w = finish.tile([P, CH], F32, name="shifted")
-            nc.vector.scalar_tensor_tensor(
-                out=w[:].rearrange("p (x e) -> p x e", e=2),
-                in0=bank[:].rearrange("p (e x) -> p x e", e=2),
-                scalar=-0.5,
-                in1=bias_neg[:].rearrange("p (x e) -> p x e", e=2),
-                op0=ALU.mult,
-                op1=ALU.add,
-            )
+            for cols in parts(n):
+                pairs = slice(cols.start // 2, cols.stop // 2)
+                nc.vector.scalar_tensor_tensor(
+                    out=w[:, cols].rearrange("p (x e) -> p x e", e=2),
+                    in0=bank[:].rearrange("p (e x) -> p x e", e=2)[:, pairs, :],
+                    scalar=-0.5,
+                    in1=bias_neg[:, cols].rearrange("p (x e) -> p x e", e=2),
+                    op0=ALU.mult,
+                    op1=ALU.add,
+                )
             shifted[n] = w
 
+        def on_gpsimd(n):
+            return GFIRST <= n < TILES - 1 and n % GMOD == 0
+
         def relu(n):
+            w = shifted[n]
+            if on_gpsimd(n):
+                above = finish.tile([P, CH], F32, name="above")
+                nc.scalar.activation(out=above[:], in_=w[:], func=ACT.Relu, scale=-1.0)
+                below = finish.tile([P, CH], F32, name="below")
+                nc.scalar.activation(out=below[:], in_=w[:], func=ACT.Relu, bias=-2.0 * THRESHOLD)
+                positive[n] = (above, below)
+                return
             a = finish.tile([P, CH], F32, name="positive")
-            nc.scalar.activation(out=a[:], in_=shifted[n][:], func=ACT.Relu)
+            for cols in parts(n):
+                nc.scalar.activation(out=a[:, cols], in_=w[:, cols], func=ACT.Relu)
             positive[n] = a
 
+        def parts(n):
+            return halves if n == TILES - 1 and SPLIT else (everything,)
+
         def finish_tile(n):
-            result = finish.tile([P, CH], F32, name="result")
-            nc.vector.scalar_tensor_tensor(
-                out=result[:],
-                in0=positive[n][:],
-                scalar=2.0 * THRESHOLD,
-                in1=shifted[n][:],
-                op0=ALU.min,
-                op1=ALU.subtract,
-            )
-            nc.sync.dma_start(out=out_dram[:, n, :], in_=result[:])
+            result = finish.tile([P, CH], F32, name="result", bufs=8)
+            if on_gpsimd(n):
+                above, below = positive[n]
+                nc.gpsimd.tensor_tensor(out=result[:], in0=above[:], in1=below[:], op=ALU.subtract)
+                nc.sync.dma_start(out=out_dram[:, n, :], in_=result[:])
+                return
+            for cols in parts(n):
+                nc.vector.scalar_tensor_tensor(
+                    out=result[:, cols],
+                    in0=positive[n][:, cols],
+                    scalar=2.0 * THRESHOLD,
+                    in1=shifted[n][:, cols],
+                    op0=ALU.min,
+                    op1=ALU.subtract,
+                )
+                nc.sync.dma_start(out=out_dram[:, n, cols], in_=result[:, cols])
 
-        pending = []
+        QUARTERS = 4
 
-        def finish_one():
-            if pending:
-                finish_tile(pending.pop(0))
+        def quarter(r, h):
+            return slice(h * SIZES[r] * P // 4, (h + 1) * SIZES[r] * P // 4)
 
-        def half_steps(r):
-            a, b = half_of(r, 0), half_of(r, 1)
-            return [
-                lambda: interleave(r, a, nc.vector.tensor_copy),
-                lambda: interleave(r, b, nc.vector.tensor_copy),
-                lambda: quantise_o(r, 0),
-                lambda: quantise_o(r, 1),
-            ]
+        def warm_up():
+            if WARM:
+                bank = psum.tile([P, CH], F32, tag="bank")
+                for j in range(WARM):
+                    nc.tensor.matmul(out=bank[:], lhsT=ones[:], rhs=bias_rows[:], start=True, stop=True)
 
-        def iteration(i):
-            transposing = i < ROUNDS
-            in_first = 1 <= i <= ROUNDS
-            in_second = i >= 2
-            if transposing:
-                start_round(i)
-                transpose_input(i, 0)
-            if pending:
-                relu(pending[-1])
-            while len(pending) > 1:
-                finish_one()
-            if transposing:
-                quantise_input(i, 0)
-            finish_one()
-            steps = []
-            if in_first:
-                for t in range(PACK):
-                    add_bias(i - 1, t, first_layer(i - 1, t))
-                steps = half_steps(i - 1)
-            z = SIZES[i - 2] if in_second else 0
-            for j in range(z):
-                n = FIRST[i - 2] + j
-                if j == z // 2 and transposing:
-                    transpose_input(i, 1)
-                if j == z - 1 and transposing:
-                    quantise_input(i, 1)
-                leave(n, second_layer(i - 2, j))
-                if j < z - 1:
-                    relu(n)
-                if steps:
-                    steps.pop(0)()
-                if j >= z // 2 or not transposing:
-                    finish_one()
-                pending.append(n)
-            for step in steps:
-                step()
-            if transposing and z == 0:
-                transpose_input(i, 1)
-                quantise_input(i, 1)
+        x_banks = {}
+        l1_banks = {}
+        left = []
+        gone = []
+        ready = []
 
+        def later(queue, action):
+            if queue:
+                action(queue.pop(0))
+
+        def exists(r):
+            return 0 <= r < ROUNDS
+
+        def x_copy(r, which, half):
+            copy_out(r, which, *x_banks.pop((r, which, half)))
+
+        def step(i, s):
+            a, b, c = i - 1, i - 2, i - 3
+            if s == 0 and i == 0:
+                pass
+            if s == XK[1] and exists(i + XK[0]):
+                transpose_input(i + XK[0], 0)
+            if s == XN[1] and exists(i + XN[0]):
+                transpose_input(i + XN[0], 1)
+            if exists(a):
+                l1_banks[a, s] = first_layer(a, s)
+            if s == 0 and (b, 3) in l1_banks:
+                add_bias(b, 3, l1_banks.pop((b, 3)))
+            if s > 0 and (a, s - 1) in l1_banks:
+                add_bias(a, s - 1, l1_banks.pop((a, s - 1)))
+            for which, (dr, ds) in ((0, CK), (1, CN)):
+                for half in range(2):
+                    at = ds + half
+                    r = i + dr - at // 4
+                    if at % 4 == s and (r, which, half) in x_banks:
+                        x_copy(r, which, half)
+            if gone:
+                n = gone.pop(0)
+                relu(n)
+                ready.append(n)
+            if left:
+                n, bank = left.pop(0)
+                leave(n, bank)
+                gone.append(n)
+            for which, (dr, ds) in ((0, CK), (1, CN)):
+                for half in range(2):
+                    at = ds + half + QLAG
+                    r = i + dr - at // 4
+                    if at % 4 == s and exists(r) and r > 1 and (SIZES[r] > 2 or half == 0):
+                        quantise_input_part(r, which, half)
+            if exists(b):
+                if s == 1:
+                    interleave(b, quarter(b, 0), nc.scalar.copy)
+                if s >= 1:
+                    interleave(b, quarter(b, s), nc.scalar.copy if s in SQ else nc.vector.tensor_copy)
+                if s == OQ:
+                    quantise_o(b, 0)
+            if len(ready) > 1:
+                finish_tile(ready.pop(0))
+            if s == 0 and exists(c):
+                quantise_o(c, 1)
+            if exists(c) and s < SIZES[c]:
+                left.append((FIRST[c] + s, second_layer(c, s)))
+
+        prepare_biases()
         combine(combined_wa, ALU.add, 0)
         group(grouped_wa, combined_wa, 0, nc.scalar.copy)
         combine(combined_wb, ALU.subtract, 0)
-        combine(combined_wa, ALU.add, 1)
-        group(grouped_wa, combined_wa, 1, nc.scalar.copy)
         group(grouped_wb, combined_wb, 0, nc.vector.tensor_copy)
-        combine(combined_wb, ALU.subtract, 1)
+        transpose_input(0, 0)
+        transpose_input(0, 1)
+        for which in range(2):
+            for half in range((SIZES[0] + 1) // 2):
+                x_copy(0, which, half)
         quantise_weight(grouped_wb, wb, 0)
         quantise_weight(grouped_wa, wa, 0)
+        combine(combined_wa, ALU.add, 1)
+        group(grouped_wa, combined_wa, 1, nc.scalar.copy)
+        quantise_input(0, 0)
+        combine(combined_wb, ALU.subtract, 1)
+        quantise_input(0, 1)
         group(grouped_wb, combined_wb, 1, nc.vector.tensor_copy)
-        prepare_biases()
+        warm_up()
+        l1_banks[0, 0] = first_layer(0, 0)
+        l1_banks[0, 1] = first_layer(0, 1)
+        transpose_input(1, 0)
+        transpose_input(1, 1)
+        add_bias(0, 0, l1_banks.pop((0, 0)))
+        add_bias(0, 1, l1_banks.pop((0, 1)))
         quantise_weight(grouped_wb, wb, 1)
         quantise_weight(grouped_wa, wa, 1)
-        for i in range(ROUNDS + 2):
-            iteration(i)
-        relu(pending[-1])
-        while pending:
-            finish_one()
+        for half in range((SIZES[1] + 1) // 2):
+            x_copy(1, 0, half)
+        quantise_input(1, 0)
+        l1_banks[0, 2] = first_layer(0, 2)
+        l1_banks[0, 3] = first_layer(0, 3)
+        add_bias(0, 2, l1_banks.pop((0, 2)))
+        for half in range((SIZES[1] + 1) // 2):
+            x_copy(1, 1, half)
+        quantise_input(1, 1)
+        transpose_input(2, 0)
+        transpose_input(2, 1)
+        if BIAS3:
+            add_bias(0, 3, l1_banks.pop((0, 3)))
+        x_copy(2, 0, 0)
+        x_copy(2, 1, 0)
+        for i in range(2, ROUNDS + 3):
+            for s in range(4):
+                step(i, s)
+        while left or gone or ready:
+            if left:
+                n, bank = left.pop(0)
+                leave(n, bank)
+                gone.append(n)
+            if ready:
+                finish_tile(ready.pop(0))
+            if gone:
+                n = gone.pop(0)
+                relu(n)
+                ready.append(n)

@@ -33,7 +33,11 @@ BIAS3 = True
 OQ = 2
 SQ = (2,)
 GFIRST = 22
-GMOD = 2
+GPAR = 0
+GSET = (1, 3)
+WIDEQ = True
+QK = 1
+QN = 2
 SPLIT = True
 NPOS = 0
 QPOS = 2
@@ -260,16 +264,16 @@ def tile_afno2d_pb_t_kernel(tc, o1k, o1n, w2, b2, out):
             shifted[n] = w
 
         def on_gpsimd(n):
-            return GFIRST <= n < TILES - 1 and n % GMOD == 0
+            return n < TILES - 1 and (n % 4 in GSET or n >= GFIRST and n % 2 == GPAR)
 
         def relu(n):
             w = shifted[n]
             if on_gpsimd(n):
-                above = finish.tile([P, CH], F32, name="above")
-                nc.scalar.activation(out=above[:], in_=w[:], func=ACT.Relu, scale=-1.0)
-                below = finish.tile([P, CH], F32, name="below")
-                nc.scalar.activation(out=below[:], in_=w[:], func=ACT.Relu, bias=-2.0 * THRESHOLD)
-                positive[n] = (above, below)
+                c = finish.tile([P, CH], F32, name="clamped")
+                nc.vector.tensor_scalar(
+                    out=c[:], in0=w[:], scalar1=0.0, scalar2=2.0 * THRESHOLD, op0=ALU.max, op1=ALU.min
+                )
+                positive[n] = c
                 return
             a = finish.tile([P, CH], F32, name="positive")
             for cols in parts(n):
@@ -282,8 +286,7 @@ def tile_afno2d_pb_t_kernel(tc, o1k, o1n, w2, b2, out):
         def finish_tile(n):
             result = finish.tile([P, CH], F32, name="result", bufs=8)
             if on_gpsimd(n):
-                above, below = positive[n]
-                nc.gpsimd.tensor_tensor(out=result[:], in0=above[:], in1=below[:], op=ALU.subtract)
+                nc.gpsimd.tensor_tensor(out=result[:], in0=positive[n][:], in1=shifted[n][:], op=ALU.subtract)
                 nc.sync.dma_start(out=out_dram[:, n, :], in_=result[:])
                 return
             for cols in parts(n):
@@ -352,7 +355,12 @@ def tile_afno2d_pb_t_kernel(tc, o1k, o1n, w2, b2, out):
                 n, bank = left.pop(0)
                 leave(n, bank)
                 gone.append(n)
-            for which, (dr, ds) in ((0, CK), (1, CN)):
+            if WIDEQ:
+                if s == QK and exists(i) and i > 1:
+                    quantise_input(i, 0)
+                if s == QN and exists(i) and i > 1:
+                    quantise_input(i, 1)
+            for which, (dr, ds) in () if WIDEQ else ((0, CK), (1, CN)):
                 for half in range(2):
                     at = ds + half + QLAG
                     r = i + dr - at // 4

@@ -32,9 +32,9 @@ VX = ((1, 1, 0), (1, 1, 1))
 BIAS3 = True
 OQ = 2
 SQ = (2,)
-GFIRST = 22
+GFIRST = 100
 GPAR = 0
-GSET = (1, 3)
+GSET = ()
 WIDEQ = True
 QK = 1
 QN = 2

@@ -22,13 +22,14 @@ ROUNDS = len(SIZES)
 FIRST = tuple(sum(SIZES[:r]) for r in range(ROUNDS))
 WIDEST = max(SIZES) * P
 S_COLS = 128
-XK = (1, 3)
+XK = (1, 1)
 XN = (1, 3)
-CK = (1, 3)
+CK = (1, 1)
 CN = (1, 3)
 QLAG = 1
 WARM = 0
-VX = ((1, 1, 0), (1, 1, 1))
+LASTO = True
+VX = ((1, 1, 0), (1, 1, 1), (1, 0, 1))
 BIAS3 = True
 OQ = 2
 SQ = (2,)
@@ -36,7 +37,7 @@ GFIRST = 100
 GPAR = 0
 GSET = ()
 WIDEQ = True
-QK = 1
+QK = 0
 QN = 2
 SPLIT = True
 NPOS = 0
@@ -66,7 +67,7 @@ def tile_afno2d_pb_t_kernel(tc, o1k, o1n, w2, b2, out):
 
         bias_rows = keep.tile([P, CH], BF16)
         nc.vector.memset(bias_rows[:], 0.0)
-        nc.sync.dma_start(out=bias_rows[0:2, :], in_=b2.rearrange("i n c -> (i n) c"))
+        nc.scalar.dma_start(out=bias_rows[0:2, :], in_=b2.rearrange("i n c -> (i n) c"))
 
         w_raw = keep.tile([P, 2, PACK, CH], BF16)
         nc.sync.dma_start(
@@ -366,7 +367,17 @@ def tile_afno2d_pb_t_kernel(tc, o1k, o1n, w2, b2, out):
                     r = i + dr - at // 4
                     if at % 4 == s and exists(r) and r > 1 and (SIZES[r] > 2 or half == 0):
                         quantise_input_part(r, which, half)
-            if exists(b):
+            if b == ROUNDS - 1 and LASTO:
+                if s == 0:
+                    interleave(b, quarter(b, 0), nc.scalar.copy)
+                    interleave(b, quarter(b, 1), nc.vector.tensor_copy)
+                    interleave(b, quarter(b, 2), nc.scalar.copy)
+                if s == 1:
+                    quantise_o(b, 0)
+                    interleave(b, quarter(b, 3), nc.scalar.copy)
+                if s == 2:
+                    quantise_o(b, 1)
+            elif exists(b):
                 if s == 1:
                     interleave(b, quarter(b, 0), nc.scalar.copy)
                 if s >= 1:
@@ -375,7 +386,7 @@ def tile_afno2d_pb_t_kernel(tc, o1k, o1n, w2, b2, out):
                     quantise_o(b, 0)
             if len(ready) > 1:
                 finish_tile(ready.pop(0))
-            if s == 0 and exists(c):
+            if s == 0 and exists(c) and (c < ROUNDS - 1 or not LASTO):
                 quantise_o(c, 1)
             if exists(c) and s < SIZES[c]:
                 left.append((FIRST[c] + s, second_layer(c, s)))
@@ -421,6 +432,8 @@ def tile_afno2d_pb_t_kernel(tc, o1k, o1n, w2, b2, out):
         if BIAS3:
             add_bias(0, 3, l1_banks.pop((0, 3)))
         x_copy(2, 0, 0)
+        if XK[1] < 3:
+            x_copy(2, 0, 1)
         x_copy(2, 1, 0)
         for i in range(2, ROUNDS + 3):
             for s in range(4):

@@ -28,7 +28,11 @@ CK = (1, 1)
 CN = (1, 3)
 QLAG = 1
 WARM = 0
-LASTO = True
+S_PART = 320
+RLAG = 1
+SINGLES = 8
+FPAR = 0
+VIL = 2
 VX = ((1, 1, 0), (1, 1, 1), (1, 0, 1))
 BIAS3 = True
 OQ = 2
@@ -38,7 +42,7 @@ GPAR = 0
 GSET = ()
 WIDEQ = True
 QK = 0
-QN = 2
+QN = 1
 SPLIT = True
 NPOS = 0
 QPOS = 2
@@ -58,7 +62,7 @@ def tile_afno2d_pb_t_kernel(tc, o1k, o1n, w2, b2, out):
         inputs = ctx.enter_context(tc.tile_pool(name="inputs", bufs=1))
         stage = ctx.enter_context(tc.tile_pool(name="stage", bufs=3))
         quantised = ctx.enter_context(tc.tile_pool(name="quantised", bufs=5))
-        finish = ctx.enter_context(tc.tile_pool(name="finish", bufs=4))
+        finish = ctx.enter_context(tc.tile_pool(name="finish", bufs=3))
         psum = ctx.enter_context(tc.psum_pool(name="psum", bufs=8))
 
         k_dram = o1k.rearrange("b h w n c -> (b h w n) c").rearrange("(p j) c -> p j c", j=TILES)
@@ -67,13 +71,14 @@ def tile_afno2d_pb_t_kernel(tc, o1k, o1n, w2, b2, out):
 
         bias_rows = keep.tile([P, CH], BF16)
         nc.vector.memset(bias_rows[:], 0.0)
-        nc.scalar.dma_start(out=bias_rows[0:2, :], in_=b2.rearrange("i n c -> (i n) c"))
 
         w_raw = keep.tile([P, 2, PACK, CH], BF16)
         nc.sync.dma_start(
             out=w_raw[:].rearrange("p i (u e) c -> p (i u) (e c)", e=2),
             in_=w2.rearrange("i n (u p e) c -> p (i n u) (e c)", u=2, p=P, e=2),
         )
+
+        nc.sync.dma_start(out=bias_rows[0:2, :], in_=b2.rearrange("i n c -> (i n) c"))
 
         k_rounds = []
         n_rounds = []
@@ -93,19 +98,21 @@ def tile_afno2d_pb_t_kernel(tc, o1k, o1n, w2, b2, out):
         bias_neg = keep.tile([P, CH], F32)
         bias_k = keep.tile([P, 2, 2], F32)
 
-        def prepare_biases():
-            sum_bank = psum.tile([P, CH], F32, tag="bank")
-            nc.tensor.matmul(out=sum_bank[:], lhsT=ones[:], rhs=bias_rows[:], start=True, stop=True)
+        def prepare_bias_k():
             words_bank = psum.tile([P, 2, P], F32, tag="bank")
             words = bias_rows[:].bitcast(F32)
             for u in range(2):
                 nc.tensor.transpose(words_bank[:, u, :], words[:, u * P : (u + 1) * P], ident_f32[:])
-            nc.scalar.activation(
-                out=bias_neg[:], in_=sum_bank[:], func=ACT.Identity, bias=THRESHOLD, scale=-1.0
-            )
             pairs = words_bank[:].rearrange("p u r -> p (u r)").bitcast(BF16)
             nc.vector.tensor_copy(
                 out=bias_k[:], in_=pairs.rearrange("p (u x) -> p u x", u=2)[:, :, 0:2]
+            )
+
+        def prepare_bias_neg():
+            sum_bank = psum.tile([P, CH], F32, tag="bank")
+            nc.tensor.matmul(out=sum_bank[:], lhsT=ones[:], rhs=bias_rows[:], start=True, stop=True)
+            nc.vector.tensor_scalar(
+                out=bias_neg[:], in0=sum_bank[:], scalar1=-1.0, scalar2=THRESHOLD, op0=ALU.mult, op1=ALU.add
             )
 
         def new_operand(pool, name):
@@ -166,13 +173,21 @@ def tile_afno2d_pb_t_kernel(tc, o1k, o1n, w2, b2, out):
         o_q = {}
         shifted = {}
         positive = {}
+        results = {}
 
         def start_round(r):
-            x_grouped[r] = (
-                stage.tile([P, WIDEST, PACK], BF16, name="k_grouped", align_bytes=64),
-                stage.tile([P, WIDEST, PACK], BF16, name="n_grouped", align_bytes=64),
+            both = stage.tile([P, 2, WIDEST, PACK], BF16, name="x_grouped", align_bytes=64)
+            codes = quantised.tile([P, 2, CH], U32, name="x_codes", align_bytes=64)
+            scales = quantised.tile([P, 2, CH], U8, name="x_scales", align_bytes=64)
+            x_grouped[r] = (both[:, 0], both[:, 1], both)
+            x_q[r] = ((codes[:, 0], scales[:, 0]), (codes[:, 1], scales[:, 1]), codes, scales)
+
+        def quantise_both(r):
+            nc.vector.quantize_mx(
+                out=x_q[r][2][:].rearrange("p x c -> p (x c)").bitcast(FP8X4),
+                scales=x_q[r][3][:].rearrange("p x c -> p (x c)"),
+                in_=x_grouped[r][2][:].rearrange("p x r t -> p (x r t)"),
             )
-            x_q[r] = (new_operand(quantised, "k"), new_operand(quantised, "n"))
 
         def transpose_input(r, which):
             if which == 0:
@@ -191,7 +206,7 @@ def tile_afno2d_pb_t_kernel(tc, o1k, o1n, w2, b2, out):
                 x_banks[r, which, first // 2] = (first, here, bank)
 
         def copy_out(r, which, first, here, bank):
-            words = x_grouped[r][which][:].rearrange("p r t -> p (r t)").bitcast(F32)
+            words = x_grouped[r][which].rearrange("p r t -> p (r t)").bitcast(F32)
             copy = nc.vector.tensor_copy if (r, which, first // 2) in VX else nc.scalar.copy
             copy(
                 out=words[:, first * 2 * P : (first + here) * 2 * P].rearrange("p (l r u) -> p l r u", l=here, u=2),
@@ -209,7 +224,7 @@ def tile_afno2d_pb_t_kernel(tc, o1k, o1n, w2, b2, out):
                 planes[r] = stage.tile([P, PACK, WIDEST], BF16, name="planes")
                 o_grouped[r] = stage.tile([P, WIDEST, PACK], BF16, name="o_grouped", align_bytes=64)
                 o_q[r] = new_operand(quantised, "o")
-            k_q, n_q = x_q[r]
+            k_q, n_q = x_q[r][0:2]
             start = (t % 2) * HALF + (t // 2) * P
             channels = slice(start, start + P)
             bank = psum.tile([P, WIDEST], F32, tag="bank")
@@ -241,7 +256,7 @@ def tile_afno2d_pb_t_kernel(tc, o1k, o1n, w2, b2, out):
             return slice(h * width, (h + 1) * width)
 
         def second_layer(r, j):
-            k_q, n_q = x_q[r]
+            k_q, n_q = x_q[r][0:2]
             tokens = slice(j * P, (j + 1) * P)
             bank = psum.tile([P, CH], F32, tag="bank")
             multiply(bank[:], k_q, tokens, wa, everything, True, False)
@@ -251,7 +266,9 @@ def tile_afno2d_pb_t_kernel(tc, o1k, o1n, w2, b2, out):
             return bank
 
         def leave(n, bank):
-            w = finish.tile([P, CH], F32, name="shifted")
+            if n % 2 == 0:
+                shifted[n // 2] = finish.tile([P, 2, CH], F32, name="shifted")
+            w = shifted[n // 2][:, n % 2, :]
             for cols in parts(n):
                 pairs = slice(cols.start // 2, cols.stop // 2)
                 nc.vector.scalar_tensor_tensor(
@@ -262,44 +279,39 @@ def tile_afno2d_pb_t_kernel(tc, o1k, o1n, w2, b2, out):
                     op0=ALU.mult,
                     op1=ALU.add,
                 )
-            shifted[n] = w
 
-        def on_gpsimd(n):
-            return n < TILES - 1 and (n % 4 in GSET or n >= GFIRST and n % 2 == GPAR)
+        def pieces(pair):
+            if pair < SINGLES:
+                return [(slice(0, 2), everything)]
+            if pair < TILES // 2 - 1:
+                return [(slice(0, 1), everything), (slice(1, 2), everything)]
+            return [(slice(0, 1), everything), (slice(1, 2), halves[0]), (slice(1, 2), halves[1])]
 
-        def relu(n):
-            w = shifted[n]
-            if on_gpsimd(n):
-                c = finish.tile([P, CH], F32, name="clamped")
-                nc.vector.tensor_scalar(
-                    out=c[:], in0=w[:], scalar1=0.0, scalar2=2.0 * THRESHOLD, op0=ALU.max, op1=ALU.min
-                )
-                positive[n] = c
-                return
-            a = finish.tile([P, CH], F32, name="positive")
-            for cols in parts(n):
-                nc.scalar.activation(out=a[:, cols], in_=w[:, cols], func=ACT.Relu)
-            positive[n] = a
+        def relu(pair, tiles, cols):
+            if tiles.start == 0:
+                positive[pair] = finish.tile([P, 2, CH], F32, name="positive")
+            nc.scalar.activation(
+                out=positive[pair][:, tiles, cols], in_=shifted[pair][:, tiles, cols], func=ACT.Relu
+            )
 
         def parts(n):
             return halves if n == TILES - 1 and SPLIT else (everything,)
 
-        def finish_tile(n):
-            result = finish.tile([P, CH], F32, name="result", bufs=8)
-            if on_gpsimd(n):
-                nc.gpsimd.tensor_tensor(out=result[:], in0=positive[n][:], in1=shifted[n][:], op=ALU.subtract)
-                nc.sync.dma_start(out=out_dram[:, n, :], in_=result[:])
-                return
-            for cols in parts(n):
-                nc.vector.scalar_tensor_tensor(
-                    out=result[:, cols],
-                    in0=positive[n][:, cols],
-                    scalar=2.0 * THRESHOLD,
-                    in1=shifted[n][:, cols],
-                    op0=ALU.min,
-                    op1=ALU.subtract,
-                )
-                nc.sync.dma_start(out=out_dram[:, n, cols], in_=result[:, cols])
+        def finish_piece(pair, tiles, cols):
+            if tiles.start == 0:
+                results[pair] = finish.tile([P, 2, CH], F32, name="result", bufs=5)
+            nc.vector.scalar_tensor_tensor(
+                out=results[pair][:, tiles, cols],
+                in0=positive[pair][:, tiles, cols],
+                scalar=2.0 * THRESHOLD,
+                in1=shifted[pair][:, tiles, cols],
+                op0=ALU.min,
+                op1=ALU.subtract,
+            )
+            nc.sync.dma_start(
+                out=out_dram[:, 2 * pair + tiles.start : 2 * pair + tiles.stop, cols],
+                in_=results[pair][:, tiles, cols],
+            )
 
         QUARTERS = 4
 
@@ -321,6 +333,13 @@ def tile_afno2d_pb_t_kernel(tc, o1k, o1n, w2, b2, out):
         def later(queue, action):
             if queue:
                 action(queue.pop(0))
+
+        def leave_one():
+            n, bank = left.pop(0)
+            leave(n, bank)
+            for tiles, cols in pieces(n // 2):
+                if tiles.stop == n % 2 + 1:
+                    gone.append((n // 2, tiles, cols))
 
         def exists(r):
             return 0 <= r < ROUNDS
@@ -349,49 +368,35 @@ def tile_afno2d_pb_t_kernel(tc, o1k, o1n, w2, b2, out):
                     if at % 4 == s and (r, which, half) in x_banks:
                         x_copy(r, which, half)
             if gone:
-                n = gone.pop(0)
-                relu(n)
-                ready.append(n)
+                piece = gone.pop(0)
+                relu(*piece)
+                ready.append(piece)
             if left:
-                n, bank = left.pop(0)
-                leave(n, bank)
-                gone.append(n)
+                leave_one()
             if WIDEQ:
-                if s == QK and exists(i) and i > 1:
-                    quantise_input(i, 0)
                 if s == QN and exists(i) and i > 1:
-                    quantise_input(i, 1)
+                    quantise_both(i)
             for which, (dr, ds) in () if WIDEQ else ((0, CK), (1, CN)):
                 for half in range(2):
                     at = ds + half + QLAG
                     r = i + dr - at // 4
                     if at % 4 == s and exists(r) and r > 1 and (SIZES[r] > 2 or half == 0):
                         quantise_input_part(r, which, half)
-            if b == ROUNDS - 1 and LASTO:
-                if s == 0:
-                    interleave(b, quarter(b, 0), nc.scalar.copy)
-                    interleave(b, quarter(b, 1), nc.vector.tensor_copy)
-                    interleave(b, quarter(b, 2), nc.scalar.copy)
-                if s == 1:
-                    quantise_o(b, 0)
-                    interleave(b, quarter(b, 3), nc.scalar.copy)
-                if s == 2:
-                    quantise_o(b, 1)
-            elif exists(b):
-                if s == 1:
-                    interleave(b, quarter(b, 0), nc.scalar.copy)
-                if s >= 1:
-                    interleave(b, quarter(b, s), nc.scalar.copy if s in SQ else nc.vector.tensor_copy)
-                if s == OQ:
-                    quantise_o(b, 0)
-            if len(ready) > 1:
-                finish_tile(ready.pop(0))
-            if s == 0 and exists(c) and (c < ROUNDS - 1 or not LASTO):
-                quantise_o(c, 1)
-            if exists(c) and s < SIZES[c]:
-                left.append((FIRST[c] + s, second_layer(c, s)))
+            if exists(b):
+                width = SIZES[b] * P
+                if s == 1 - (b == ROUNDS - 1):
+                    interleave(b, slice(0, S_PART * SIZES[b] // 4), nc.scalar.copy)
+                if s == VIL - (b == ROUNDS - 1):
+                    interleave(b, slice(S_PART * SIZES[b] // 4, width), nc.vector.tensor_copy)
+                if s == 3 - (b == ROUNDS - 1):
+                    quantise(o_grouped[b], o_q[b], slice(0, width))
+            if len(ready) > RLAG or (ready and s % 2 == FPAR):
+                finish_piece(*ready.pop(0))
+            per = SIZES[c] * (s + 1) // 4 - SIZES[c] * s // 4 if exists(c) else 0
+            for j in range(per):
+                n = SIZES[c] * s // 4 + j
+                left.append((FIRST[c] + n, second_layer(c, n)))
 
-        prepare_biases()
         combine(combined_wa, ALU.add, 0)
         group(grouped_wa, combined_wa, 0, nc.scalar.copy)
         combine(combined_wb, ALU.subtract, 0)
@@ -408,6 +413,7 @@ def tile_afno2d_pb_t_kernel(tc, o1k, o1n, w2, b2, out):
         quantise_input(0, 0)
         combine(combined_wb, ALU.subtract, 1)
         quantise_input(0, 1)
+        prepare_bias_k()
         group(grouped_wb, combined_wb, 1, nc.vector.tensor_copy)
         warm_up()
         l1_banks[0, 0] = first_layer(0, 0)
@@ -427,6 +433,7 @@ def tile_afno2d_pb_t_kernel(tc, o1k, o1n, w2, b2, out):
         for half in range((SIZES[1] + 1) // 2):
             x_copy(1, 1, half)
         quantise_input(1, 1)
+        prepare_bias_neg()
         transpose_input(2, 0)
         transpose_input(2, 1)
         if BIAS3:
@@ -440,12 +447,10 @@ def tile_afno2d_pb_t_kernel(tc, o1k, o1n, w2, b2, out):
                 step(i, s)
         while left or gone or ready:
             if left:
-                n, bank = left.pop(0)
-                leave(n, bank)
-                gone.append(n)
+                leave_one()
             if ready:
-                finish_tile(ready.pop(0))
+                finish_piece(*ready.pop(0))
             if gone:
-                n = gone.pop(0)
-                relu(n)
-                ready.append(n)
+                piece = gone.pop(0)
+                relu(*piece)
+                ready.append(piece)

@@ -17,7 +17,7 @@ CH = P * PACK
 HALF = CH // 2
 TOKENS = 64 * 64
 TILES = TOKENS // P
-SIZES = (4,)*8
+SIZES = (4,) * 8
 ROUNDS = len(SIZES)
 FIRST = tuple(sum(SIZES[:r]) for r in range(ROUNDS))
 WIDEST = max(SIZES) * P
@@ -27,12 +27,14 @@ XN = (1, 3)
 CK = (1, 1)
 CN = (1, 3)
 QLAG = 1
-WARM = 0
 S_PART = 320
 RLAG = 1
 SINGLES = 8
 FPAR = 0
 VIL = 2
+SFULL = 1
+SHN = 2
+QE = 0
 VX = ((1, 1, 0), (1, 1, 1), (1, 0, 1))
 BIAS3 = True
 OQ = 2
@@ -183,6 +185,10 @@ def tile_afno2d_pb_t_kernel(tc, o1k, o1n, w2, b2, out):
             x_q[r] = ((codes[:, 0], scales[:, 0]), (codes[:, 1], scales[:, 1]), codes, scales)
 
         def quantise_both(r):
+            if SIZES[r] * P < WIDEST:
+                quantise_input(r, 0)
+                quantise_input(r, 1)
+                return
             nc.vector.quantize_mx(
                 out=x_q[r][2][:].rearrange("p x c -> p (x c)").bitcast(FP8X4),
                 scales=x_q[r][3][:].rearrange("p x c -> p (x c)"),
@@ -318,12 +324,6 @@ def tile_afno2d_pb_t_kernel(tc, o1k, o1n, w2, b2, out):
         def quarter(r, h):
             return slice(h * SIZES[r] * P // 4, (h + 1) * SIZES[r] * P // 4)
 
-        def warm_up():
-            if WARM:
-                bank = psum.tile([P, CH], F32, tag="bank")
-                for j in range(WARM):
-                    nc.tensor.matmul(out=bank[:], lhsT=ones[:], rhs=bias_rows[:], start=True, stop=True)
-
         x_banks = {}
         l1_banks = {}
         left = []
@@ -384,11 +384,13 @@ def tile_afno2d_pb_t_kernel(tc, o1k, o1n, w2, b2, out):
                         quantise_input_part(r, which, half)
             if exists(b):
                 width = SIZES[b] * P
-                if s == 1 - (b == ROUNDS - 1):
-                    interleave(b, slice(0, S_PART * SIZES[b] // 4), nc.scalar.copy)
-                if s == VIL - (b == ROUNDS - 1):
-                    interleave(b, slice(S_PART * SIZES[b] // 4, width), nc.vector.tensor_copy)
-                if s == 3 - (b == ROUNDS - 1):
+                early = 1 if b >= ROUNDS - SHN else 0
+                s_width = width if b >= ROUNDS - SFULL else S_PART * SIZES[b] // 4
+                if s == 1 - early:
+                    interleave(b, slice(0, s_width), nc.scalar.copy)
+                if s == VIL - early and s_width < width:
+                    interleave(b, slice(s_width, width), nc.vector.tensor_copy)
+                if s == 3 - early - (QE if early else 0):
                     quantise(o_grouped[b], o_q[b], slice(0, width))
             if len(ready) > RLAG or (ready and s % 2 == FPAR):
                 finish_piece(*ready.pop(0))
@@ -415,7 +417,6 @@ def tile_afno2d_pb_t_kernel(tc, o1k, o1n, w2, b2, out):
         quantise_input(0, 1)
         prepare_bias_k()
         group(grouped_wb, combined_wb, 1, nc.vector.tensor_copy)
-        warm_up()
         l1_banks[0, 0] = first_layer(0, 0)
         l1_banks[0, 1] = first_layer(0, 1)
         transpose_input(1, 0)

from contextlib import ExitStack

import concourse.mybir as mybir
from concourse.masks import make_identity

F32 = mybir.dt.float32
BF16 = mybir.dt.bfloat16
U32 = mybir.dt.uint32
U8 = mybir.dt.uint8
FP8X4 = mybir.dt.float8_e4m3fn_x4
ALU = mybir.AluOpType
ACT = mybir.ActivationFunctionType

P = 128
PACK = 4
CH = P * PACK
HALF = CH // 2
TOKENS = 64 * 64
TILES = TOKENS // P
SIZES = (4,) * 8
ROUNDS = len(SIZES)
FIRST = tuple(sum(SIZES[:r]) for r in range(ROUNDS))
WIDEST = max(SIZES) * P
S_COLS = 128
XK = (1, 1)
XN = (1, 3)
CK = (1, 1)
CN = (1, 3)
QLAG = 1
S_PART = 320
RLAG = 1
SINGLES = 8
FPAR = 0
VIL = 2
SFULL = 1
SHN = 2
QE = 0
VX = ((1, 1, 0), (1, 1, 1), (1, 0, 1))
BIAS3 = True
OQ = 2
SQ = (2,)
GFIRST = 100
GPAR = 0
GSET = ()
WIDEQ = True
QK = 0
QN = 1
SPLIT = True
NPOS = 0
QPOS = 2
MERGE = False
KQPOS = 1
FPOS = 2
THRESHOLD = 0.01

FLOPS = 4 * 2 * TOKENS * CH * CH


def tile_afno2d_pb_t_kernel(tc, o1k, o1n, w2, b2, out):
    nc = tc.nc
    with ExitStack() as ctx:
        ctx.enter_context(tc.manual_schedule())
        keep = ctx.enter_context(tc.tile_pool(name="keep", bufs=1))
        inputs = ctx.enter_context(tc.tile_pool(name="inputs", bufs=1))
        stage = ctx.enter_context(tc.tile_pool(name="stage", bufs=3))
        quantised = ctx.enter_context(tc.tile_pool(name="quantised", bufs=5))
        finish = ctx.enter_context(tc.tile_pool(name="finish", bufs=3))
        psum = ctx.enter_context(tc.psum_pool(name="psum", bufs=8))

        k_dram = o1k.rearrange("b h w n c -> (b h w n) c").rearrange("(p j) c -> p j c", j=TILES)
        n_dram = o1n.rearrange("b h w n c -> (b h w n) c").rearrange("(p j) c -> p j c", j=TILES)
        out_dram = out.rearrange("b h w c -> (b h w) c").rearrange("(p j) c -> p j c", j=TILES)

        bias_rows = keep.tile([P, CH], BF16)
        nc.vector.memset(bias_rows[:], 0.0)

        w_raw = keep.tile([P, 2, PACK, CH], BF16)
        nc.sync.dma_start(
            out=w_raw[:].rearrange("p i (u e) c -> p (i u) (e c)", e=2),
            in_=w2.rearrange("i n (u p e) c -> p (i n u) (e c)", u=2, p=P, e=2),
        )

        nc.sync.dma_start(out=bias_rows[0:2, :], in_=b2.rearrange("i n c -> (i n) c"))

        k_rounds = []
        n_rounds = []
        for r in range(ROUNDS):
            tiles_of_round = slice(FIRST[r], FIRST[r] + SIZES[r])
            k_in = inputs.tile([P, SIZES[r], CH], BF16, name="k_in%d" % r)
            nc.sync.dma_start(out=k_in[:], in_=k_dram[:, tiles_of_round, :])
            n_in = inputs.tile([P, SIZES[r], CH], BF16, name="n_in%d" % r)
            nc.sync.dma_start(out=n_in[:], in_=n_dram[:, tiles_of_round, :])
            k_rounds.append(k_in)
            n_rounds.append(n_in)

        ident_f32 = keep.tile([P, P], F32)
        make_identity(nc, ident_f32[:])
        ones = keep.tile([P, P], BF16)
        nc.vector.memset(ones[:], 1.0)
        bias_neg = keep.tile([P, CH], F32)
        bias_k = keep.tile([P, 2, 2], F32)

        def prepare_bias_k():
            words_bank = psum.tile([P, 2, P], F32, tag="bank")
            words = bias_rows[:].bitcast(F32)
            for u in range(2):
                nc.tensor.transpose(words_bank[:, u, :], words[:, u * P : (u + 1) * P], ident_f32[:])
            pairs = words_bank[:].rearrange("p u r -> p (u r)").bitcast(BF16)
            nc.vector.tensor_copy(
                out=bias_k[:], in_=pairs.rearrange("p (u x) -> p u x", u=2)[:, :, 0:2]
            )

        def prepare_bias_neg():
            sum_bank = psum.tile([P, CH], F32, tag="bank")
            nc.tensor.matmul(out=sum_bank[:], lhsT=ones[:], rhs=bias_rows[:], start=True, stop=True)
            nc.vector.tensor_scalar(
                out=bias_neg[:], in0=sum_bank[:], scalar1=-1.0, scalar2=THRESHOLD, op0=ALU.mult, op1=ALU.add
            )

        def new_operand(pool, name):
            codes = pool.tile([P, CH], U32, name=name + "_codes", align_bytes=64)
            scales = pool.tile([P, CH], U8, name=name + "_scales", align_bytes=64)
            return codes, scales

        def quantise(grouped, operand, cols):
            nc.vector.quantize_mx(
                out=operand[0][:, cols].bitcast(FP8X4),
                scales=operand[1][:, cols],
                in_=grouped[:, cols, :].rearrange("p w t -> p (w t)"),
            )

        def multiply(bank, stationary, stationary_cols, moving, moving_cols, start, stop):
            nc.tensor.matmul_mx(
                out=bank,
                lhsT=stationary[0][:, stationary_cols].bitcast(FP8X4),
                lhsT_scale=stationary[1][:, stationary_cols],
                rhs=moving[0][:, moving_cols].bitcast(FP8X4),
                rhs_scale=moving[1][:, moving_cols],
                start=start,
                stop=stop,
            )

        everything = slice(0, CH)
        halves = (slice(0, HALF), slice(HALF, CH))
        wa = new_operand(keep, "wa")
        wb = new_operand(keep, "wb")
        combined_wa = keep.tile([P, PACK, CH], BF16)
        combined_wb = keep.tile([P, PACK, CH], BF16)
        grouped_wa = keep.tile([P, CH, PACK], BF16, align_bytes=64)
        grouped_wb = keep.tile([P, CH, PACK], BF16, align_bytes=64)

        def combine(combined, op, u):
            nc.vector.tensor_tensor(
                out=combined[:, :, halves[u]],
                in0=w_raw[:, 0, :, halves[u]],
                in1=w_raw[:, 1, :, halves[u]],
                op=op,
            )

        def group(grouped, combined, u, copy):
            copy(
                out=grouped[:].rearrange("p (e x) t -> p e x t", e=2)[:, :, u * P : (u + 1) * P, :],
                in_=combined[:, :, halves[u]].rearrange("p t (m e) -> p e m t", e=2),
            )

        def quantise_weight(grouped, operand, u):
            for e in range(2):
                start = e * HALF + u * P
                quantise(grouped, operand, slice(start, start + P))

        x_grouped = {}
        x_q = {}
        planes = {}
        o_grouped = {}
        o_q = {}
        shifted = {}
        positive = {}
        results = {}

        def start_round(r):
            both = stage.tile([P, 2, WIDEST, PACK], BF16, name="x_grouped", align_bytes=64)
            codes = quantised.tile([P, 2, CH], U32, name="x_codes", align_bytes=64)
            scales = quantised.tile([P, 2, CH], U8, name="x_scales", align_bytes=64)
            x_grouped[r] = (both[:, 0], both[:, 1], both)
            x_q[r] = ((codes[:, 0], scales[:, 0]), (codes[:, 1], scales[:, 1]), codes, scales)

        def quantise_both(r):
            if SIZES[r] * P < WIDEST:
                quantise_input(r, 0)
                quantise_input(r, 1)
                return
            nc.vector.quantize_mx(
                out=x_q[r][2][:].rearrange("p x c -> p (x c)").bitcast(FP8X4),
                scales=x_q[r][3][:].rearrange("p x c -> p (x c)"),
                in_=x_grouped[r][2][:].rearrange("p x r t -> p (x r t)"),
            )

        def transpose_input(r, which):
            if which == 0:
                start_round(r)
            words = (k_rounds, n_rounds)[which][r][:].bitcast(F32)
            for first in range(0, SIZES[r], 2):
                here = min(2, SIZES[r] - first)
                bank = psum.tile([P, 2, 2, P], F32, tag="bank")
                for l in range(here):
                    for u in range(2):
                        nc.tensor.transpose(
                            bank[:, l, u, :],
                            words[:, first + l, u * P : (u + 1) * P],
                            ident_f32[:],
                        )
                x_banks[r, which, first // 2] = (first, here, bank)

        def copy_out(r, which, first, here, bank):
            words = x_grouped[r][which].rearrange("p r t -> p (r t)").bitcast(F32)
            copy = nc.vector.tensor_copy if (r, which, first // 2) in VX else nc.scalar.copy
            copy(
                out=words[:, first * 2 * P : (first + here) * 2 * P].rearrange("p (l r u) -> p l r u", l=here, u=2),
                in_=bank[:, 0:here].rearrange("p l u r -> p l r u"),
            )

        def quantise_input(r, which):
            quantise(x_grouped[r][which], x_q[r][which], slice(0, SIZES[r] * P))

        def quantise_input_part(r, which, half):
            quantise(x_grouped[r][which], x_q[r][which], slice(half * 2 * P, min((half + 1) * 2, SIZES[r]) * P))

        def first_layer(r, t):
            if t == 0:
                planes[r] = stage.tile([P, PACK, WIDEST], BF16, name="planes")
                o_grouped[r] = stage.tile([P, WIDEST, PACK], BF16, name="o_grouped", align_bytes=64)
                o_q[r] = new_operand(quantised, "o")
            k_q, n_q = x_q[r][0:2]
            start = (t % 2) * HALF + (t // 2) * P
            channels = slice(start, start + P)
            bank = psum.tile([P, WIDEST], F32, tag="bank")
            tokens = slice(0, SIZES[r] * P)
            multiply(bank[:, tokens], wa, channels, k_q, tokens, True, False)
            multiply(bank[:, tokens], wb, channels, n_q, tokens, False, True)
            return bank

        def add_bias(r, t, bank):
            nc.scalar.activation(
                out=planes[r][:, t, 0 : SIZES[r] * P],
                in_=bank[:, 0 : SIZES[r] * P],
                func=ACT.Identity,
                bias=bias_k[:, t // 2, t % 2 : t % 2 + 1],
                scale=0.5,
            )

        def interleave(r, cols, copy):
            copy(
                out=o_grouped[r][:, cols, :].rearrange("p (c i) t -> p c t i", i=4),
                in_=planes[r][:, :, cols].rearrange("p t (c i) -> p c t i", i=4),
            )

        def quantise_o(r, h):
            quantise(o_grouped[r], o_q[r], half_of(r, h))

        def half_of(r, h):
            width = SIZES[r] * P // 2
            return slice(h * width, (h + 1) * width)

        def second_layer(r, j):
            k_q, n_q = x_q[r][0:2]
            tokens = slice(j * P, (j + 1) * P)
            bank = psum.tile([P, CH], F32, tag="bank")
            multiply(bank[:], k_q, tokens, wa, everything, True, False)
            multiply(bank[:], n_q, tokens, wb, everything, False, False)
            multiply(bank[:], n_q, tokens, wa, everything, False, False)
            multiply(bank[:], o_q[r], tokens, wb, everything, False, True)
            return bank

        def leave(n, bank):
            if n % 2 == 0:
                shifted[n // 2] = finish.tile([P, 2, CH], F32, name="shifted")
            w = shifted[n // 2][:, n % 2, :]
            for cols in parts(n):
                pairs = slice(cols.start // 2, cols.stop // 2)
                nc.vector.scalar_tensor_tensor(
                    out=w[:, cols].rearrange("p (x e) -> p x e", e=2),
                    in0=bank[:].rearrange("p (e x) -> p x e", e=2)[:, pairs, :],
                    scalar=-0.5,
                    in1=bias_neg[:, cols].rearrange("p (x e) -> p x e", e=2),
                    op0=ALU.mult,
                    op1=ALU.add,
                )

        def pieces(pair):
            if pair < SINGLES:
                return [(slice(0, 2), everything)]
            if pair < TILES // 2 - 1:
                return [(slice(0, 1), everything), (slice(1, 2), everything)]
            return [(slice(0, 1), everything), (slice(1, 2), halves[0]), (slice(1, 2), halves[1])]

        def relu(pair, tiles, cols):
            if tiles.start == 0:
                positive[pair] = finish.tile([P, 2, CH], F32, name="positive")
            nc.scalar.activation(
                out=positive[pair][:, tiles, cols], in_=shifted[pair][:, tiles, cols], func=ACT.Relu
            )

        def parts(n):
            return halves if n == TILES - 1 and SPLIT else (everything,)

        def finish_piece(pair, tiles, cols):
            if tiles.start == 0:
                results[pair] = finish.tile([P, 2, CH], F32, name="result", bufs=5)
            nc.vector.scalar_tensor_tensor(
                out=results[pair][:, tiles, cols],
                in0=positive[pair][:, tiles, cols],
                scalar=2.0 * THRESHOLD,
                in1=shifted[pair][:, tiles, cols],
                op0=ALU.min,
                op1=ALU.subtract,
            )
            nc.sync.dma_start(
                out=out_dram[:, 2 * pair + tiles.start : 2 * pair + tiles.stop, cols],
                in_=results[pair][:, tiles, cols],
            )

        QUARTERS = 4

        def quarter(r, h):
            return slice(h * SIZES[r] * P // 4, (h + 1) * SIZES[r] * P // 4)

        x_banks = {}
        l1_banks = {}
        left = []
        gone = []
        ready = []

        def later(queue, action):
            if queue:
                action(queue.pop(0))

        def leave_one():
            n, bank = left.pop(0)
            leave(n, bank)
            for tiles, cols in pieces(n // 2):
                if tiles.stop == n % 2 + 1:
                    gone.append((n // 2, tiles, cols))

        def exists(r):
            return 0 <= r < ROUNDS

        def x_copy(r, which, half):
            copy_out(r, which, *x_banks.pop((r, which, half)))

        def step(i, s):
            a, b, c = i - 1, i - 2, i - 3
            if s == 0 and i == 0:
                pass
            if s == XK[1] and exists(i + XK[0]):
                transpose_input(i + XK[0], 0)
            if s == XN[1] and exists(i + XN[0]):
                transpose_input(i + XN[0], 1)
            if exists(a):
                l1_banks[a, s] = first_layer(a, s)
            if s == 0 and (b, 3) in l1_banks:
                add_bias(b, 3, l1_banks.pop((b, 3)))
            if s > 0 and (a, s - 1) in l1_banks:
                add_bias(a, s - 1, l1_banks.pop((a, s - 1)))
            for which, (dr, ds) in ((0, CK), (1, CN)):
                for half in range(2):
                    at = ds + half
                    r = i + dr - at // 4
                    if at % 4 == s and (r, which, half) in x_banks:
                        x_copy(r, which, half)
            if gone:
                piece = gone.pop(0)
                relu(*piece)
                ready.append(piece)
            if left:
                leave_one()
            if WIDEQ:
                if s == QN and exists(i) and i > 1:
                    quantise_both(i)
            for which, (dr, ds) in () if WIDEQ else ((0, CK), (1, CN)):
                for half in range(2):
                    at = ds + half + QLAG
                    r = i + dr - at // 4
                    if at % 4 == s and exists(r) and r > 1 and (SIZES[r] > 2 or half == 0):
                        quantise_input_part(r, which, half)
            if exists(b):
                width = SIZES[b] * P
                early = 1 if b >= ROUNDS - SHN else 0
                s_width = width if b >= ROUNDS - SFULL else S_PART * SIZES[b] // 4
                if s == 1 - early:
                    interleave(b, slice(0, s_width), nc.scalar.copy)
                if s == VIL - early and s_width < width:
                    interleave(b, slice(s_width, width), nc.vector.tensor_copy)
                if s == 3 - early - (QE if early else 0):
                    quantise(o_grouped[b], o_q[b], slice(0, width))
            if len(ready) > RLAG or (ready and s % 2 == FPAR):
                finish_piece(*ready.pop(0))
            per = SIZES[c] * (s + 1) // 4 - SIZES[c] * s // 4 if exists(c) else 0
            for j in range(per):
                n = SIZES[c] * s // 4 + j
                left.append((FIRST[c] + n, second_layer(c, n)))

        combine(combined_wa, ALU.add, 0)
        group(grouped_wa, combined_wa, 0, nc.scalar.copy)
        combine(combined_wb, ALU.subtract, 0)
        group(grouped_wb, combined_wb, 0, nc.vector.tensor_copy)
        transpose_input(0, 0)
        transpose_input(0, 1)
        for which in range(2):
            for half in range((SIZES[0] + 1) // 2):
                x_copy(0, which, half)
        quantise_weight(grouped_wb, wb, 0)
        quantise_weight(grouped_wa, wa, 0)
        combine(combined_wa, ALU.add, 1)
        group(grouped_wa, combined_wa, 1, nc.scalar.copy)
        quantise_input(0, 0)
        combine(combined_wb, ALU.subtract, 1)
        quantise_input(0, 1)
        prepare_bias_k()
        group(grouped_wb, combined_wb, 1, nc.vector.tensor_copy)
        l1_banks[0, 0] = first_layer(0, 0)
        l1_banks[0, 1] = first_layer(0, 1)
        transpose_input(1, 0)
        transpose_input(1, 1)
        add_bias(0, 0, l1_banks.pop((0, 0)))
        add_bias(0, 1, l1_banks.pop((0, 1)))
        quantise_weight(grouped_wb, wb, 1)
        quantise_weight(grouped_wa, wa, 1)
        for half in range((SIZES[1] + 1) // 2):
            x_copy(1, 0, half)
        quantise_input(1, 0)
        l1_banks[0, 2] = first_layer(0, 2)
        l1_banks[0, 3] = first_layer(0, 3)
        add_bias(0, 2, l1_banks.pop((0, 2)))
        for half in range((SIZES[1] + 1) // 2):
            x_copy(1, 1, half)
        quantise_input(1, 1)
        prepare_bias_neg()
        transpose_input(2, 0)
        transpose_input(2, 1)
        if BIAS3:
            add_bias(0, 3, l1_banks.pop((0, 3)))
        x_copy(2, 0, 0)
        if XK[1] < 3:
            x_copy(2, 0, 1)
        x_copy(2, 1, 0)
        for i in range(2, ROUNDS + 3):
            for s in range(4):
                step(i, s)
        while left or gone or ready:
            if left:
                leave_one()
            if ready:
                finish_piece(*ready.pop(0))
            if gone:
                piece = gone.pop(0)
                relu(*piece)
                ready.append(piece)
